import numpy as np
import ml_dtypes


def mxq(x, axis, fmt="e4m3"):
    dtype, down = {"e4m3": (ml_dtypes.float8_e4m3fn, 7), "e5m2": (ml_dtypes.float8_e5m2, 14)}[fmt]
    v = np.moveaxis(np.asarray(x, np.float32).astype(ml_dtypes.bfloat16).astype(np.float64), axis, -1)
    blocks = v.reshape(v.shape[:-1] + (-1, 32))
    amax = np.abs(blocks).max(-1, keepdims=True)
    byte = np.maximum(np.where(amax > 0, np.frexp(amax)[1] - 1 + 127, 0) - down, 1)
    scale = np.exp2(byte - 127.0)
    codes = (blocks / scale).astype(np.float32).astype(dtype).astype(np.float64)
    return np.moveaxis((codes * scale).reshape(v.shape), -1, axis)


WIDE = False


def mx_kscale(k):
    if not WIDE:
        return np.ones(k)
    levels = np.array([10, -10, 5, -5, 0])
    a = np.random.permutation(np.resize(levels, k // 512 * 4)).reshape(k // 512, 4)
    idx = np.arange(k)
    return np.exp2(a[idx // 512, idx % 128 // 32])


BF16 = ml_dtypes.bfloat16


def bf(x):
    return np.asarray(x, np.float32).astype(BF16)


def f64(x):
    return np.asarray(x).astype(np.float64)


E2M1 = np.array([0.0, 0.5, 1.0, 1.5, 2.0, 3.0, 4.0, 6.0, -0.0, -0.5, -1.0, -1.5, -2.0, -3.0, -4.0, -6.0])


def pack_weight(w, fmt):
    k, n = w.shape
    w = f64(bf(w)).reshape(k // 32, 32, n)
    amax = np.abs(w).max(1)
    if fmt == "e4m3":
        byte = np.frexp(amax)[1] - 1 + 127 - 7
    else:
        mant, ex = np.frexp(amax / 6.0)
        byte = np.where(mant > 0.5, ex, ex - 1) + 127
    byte = np.clip(np.where(amax > 0, byte, 1), 1, 254)
    scaled = (w * np.exp2(127.0 - byte)[:, None, :]).reshape(k, n).astype(np.float32)
    by_word = np.ascontiguousarray(scaled.reshape(k // 512, 128, 4, n).transpose(0, 1, 3, 2))
    if fmt == "e4m3":
        words = by_word.astype(ml_dtypes.float8_e4m3fn).view(np.uint8)
    else:
        c = by_word.astype(ml_dtypes.float4_e2m1fn).view(np.uint8) & 0xF
        words = c[..., 0::2] | (c[..., 1::2] << 4)
    return np.ascontiguousarray(words), np.ascontiguousarray(byte.astype(np.uint8).reshape(k // 512, 16, n))


def unpack_weight(words, scales, fmt):
    g, p, n, _ = words.shape
    if fmt == "e4m3":
        vals = np.ascontiguousarray(words).view(ml_dtypes.float8_e4m3fn).astype(np.float64)
    else:
        nib = np.empty((g, p, n, 4), np.uint8)
        nib[..., 0::2] = words & 0xF
        nib[..., 1::2] = words >> 4
        vals = E2M1[nib]
    vals = vals * np.repeat(np.exp2(scales.astype(np.float64) - 127.0), 8, axis=1)[..., None]
    return vals.transpose(0, 1, 3, 2).reshape(g * 512, n)


B, IN, H, OUT, L, STEPS = 512, 8192, 1024, 128, 3, 3
LN_EPS = 1e-5
TAU_EPS = 1e-6
FMT = "e4m3"


def layer_norm(v, g, b):
    m = v.mean(-1, keepdims=True)
    var = ((v - m) ** 2).mean(-1, keepdims=True)
    return (v - m) / np.sqrt(var + LN_EPS) * g + b


def setup_inputs():
    r = mx_kscale(IN)
    s = mx_kscale(H)
    s = s / s.max()
    t = mx_kscale(H)
    liq_rms = np.sqrt(L * (L + 1) / 2.0)
    liq = bf(np.random.standard_normal((B, H)) * liq_rms * s)
    h = bf(np.random.standard_normal((B, H)))
    x = bf(np.random.standard_normal((B, IN)) * r)
    W_in_words, W_in_scales = pack_weight(np.ascontiguousarray((np.random.standard_normal((H, IN)) * 0.7 / np.sqrt(IN) / r).T), FMT)
    b_in = bf(np.random.standard_normal(H) * 0.3)
    W_v_words, W_v_scales = pack_weight(np.ascontiguousarray((np.random.standard_normal((H, H)) / np.sqrt(H) * t[:, None] / s).T), FMT)
    b_v = bf(np.random.standard_normal(H) * 0.5 * t)
    W_o_words, W_o_scales = pack_weight(np.ascontiguousarray((np.random.standard_normal((H, H)) / np.sqrt(H) / t).T), FMT)
    b_o = bf(np.random.standard_normal(H) * 0.5)
    g_att = bf(1.0 + 0.1 * np.random.standard_normal(H))
    beta_att = bf(np.random.standard_normal(H) * 0.3)
    tau = bf(0.5 + 0.5 * np.random.random(H))
    return {"liq": liq,
            "h": h,
            "x": x,
            "W_in_words": W_in_words,
            "W_in_scales": W_in_scales,
            "b_in": b_in,
            "W_v_words": W_v_words,
            "W_v_scales": W_v_scales,
            "b_v": b_v,
            "W_o_words": W_o_words,
            "W_o_scales": W_o_scales,
            "b_o": b_o,
            "g_att": g_att,
            "beta_att": beta_att,
            "tau": tau}


def reference(liq, h, x, W_in_words, W_in_scales, b_in, W_v_words, W_v_scales, b_v, W_o_words, W_o_scales, b_o, g_att, beta_att, tau):
    liq, h = f64(liq), f64(h)
    xin = (mxq(f64(x), 1, "e4m3") @ unpack_weight(W_in_words, W_in_scales, FMT)) + f64(b_in)
    v = (mxq(liq, 1, "e4m3") @ unpack_weight(W_v_words, W_v_scales, FMT)) + f64(b_v)
    att = (mxq(v, 1, "e4m3") @ unpack_weight(W_o_words, W_o_scales, FMT)) + f64(b_o)
    z = layer_norm(att + liq, f64(g_att), f64(beta_att))
    dh = (-h + np.tanh(z + xin)) / (f64(tau) + TAU_EPS)
    return h + dh

@@ -1,0 +1,339 @@
+from contextlib import ExitStack
+
+import concourse.mybir as mybir
+from concourse.masks import make_identity
+
+F32 = mybir.dt.float32
+BF16 = mybir.dt.bfloat16
+I32 = mybir.dt.int32
+U32 = mybir.dt.uint32
+U8 = mybir.dt.uint8
+FP8X4 = mybir.dt.float8_e4m3fn_x4
+ALU = mybir.AluOpType
+ACT = mybir.ActivationFunctionType
+
+P = 128
+B, IN, H = 512, 8192, 1024
+LN_EPS = 1e-5
+TAU_EPS = 1e-6
+ROW_TILES = B // P
+K_PASS = 4 * P
+WORDS_PASS = K_PASS // 2
+HALF = 512
+HALVES = H // HALF
+GROUPS_H = H // K_PASS
+GROUPS_IN = IN // K_PASS
+ROUND_TILES = 2
+ROUNDS = ROW_TILES // ROUND_TILES
+STEP_GROUPS = 4
+STEPS_ROUND = GROUPS_IN // STEP_GROUPS
+STEPS = ROUNDS * STEPS_ROUND
+FLIP_BANKS = 4
+FLIP_COLS = 2 * P
+X_AHEAD = 3
+
+FLOPS = 2 * B * H * (IN + H + H)
+
+ROW_BV, ROW_BO, ROW_G, ROW_BETA, ROW_BIN, ROW_TAU = 0, 1, 2, 3, 4, 5
+
+
+def half_cols(n_half):
+    return slice(HALF * n_half, HALF * (n_half + 1))
+
+
+def words_by_partition(words):
+    return words.rearrange("g p n t -> p g (n t)").bitcast(I32)
+
+
+def tile_advancedliquidneuralnetwork_pb_k_kernel(
+    tc, liq, h, x, W_in_words, W_in_scales, b_in, W_v_words, W_v_scales, b_v,
+    W_o_words, W_o_scales, b_o, g_att, beta_att, tau, out,
+):
+    nc = tc.nc
+    x_rows = x.rearrange("(p i) k -> p i k", i=ROW_TILES)
+    out_rows = out.rearrange("(p i) n -> p i n", i=ROW_TILES)
+
+    with ExitStack() as stack:
+        stack.enter_context(tc.manual_schedule())
+        keep = stack.enter_context(tc.tile_pool(name="keep", bufs=1))
+        x_pool = stack.enter_context(tc.tile_pool(name="x_pool", bufs=X_AHEAD))
+        grouped_pool = stack.enter_context(tc.tile_pool(name="grouped_pool", bufs=2))
+        operand_pool = stack.enter_context(tc.tile_pool(name="operand_pool", bufs=4))
+        sum_psum = stack.enter_context(tc.psum_pool(name="sum_psum", bufs=4))
+        work_psum = stack.enter_context(tc.psum_pool(name="work_psum", bufs=4))
+
+        win_words = keep.tile([P, GROUPS_IN, H], U32, align_bytes=64)
+        win_planes = keep.tile([P, STEPS_ROUND, H], U8, align_bytes=64)
+        ident_f32 = keep.tile([P, P], F32)
+        ident_bf = keep.tile([P, P], BF16)
+        gain = keep.tile([P, H], BF16)
+        shift = keep.tile([P, H], F32)
+        rate = keep.tile([P, H], F32)
+        z = keep.tile([P, ROW_TILES, H], F32)
+        h_rest = keep.tile([P, ROW_TILES, H], F32)
+        row_sum = keep.tile([P, ROW_TILES, HALVES], F32)
+        neg_mean = keep.tile([P, ROW_TILES], F32)
+        sq_sum = keep.tile([P, ROW_TILES], F32)
+        var_eps = keep.tile([P, ROW_TILES], F32)
+        rstd = keep.tile([P, ROW_TILES], F32)
+        neg_half = keep.tile([P, 1], F32)
+
+        def load_x(step):
+            rnd, part = divmod(step, STEPS_ROUND)
+            chunk = x_pool.tile([P, ROUND_TILES, STEP_GROUPS * K_PASS], BF16, tag="x_chunk")
+            nc.sync.dma_start(
+                out=chunk[:],
+                in_=x_rows[:, ROUND_TILES * rnd : ROUND_TILES * (rnd + 1),
+                           STEP_GROUPS * K_PASS * part : STEP_GROUPS * K_PASS * (part + 1)],
+            )
+            return chunk
+
+        def load_win(part):
+            for quad in range(4):
+                nc.sync.dma_start(
+                    out=win_planes[32 * quad : 32 * quad + 16, part, :].bitcast(I32),
+                    in_=W_in_scales[STEP_GROUPS * part : STEP_GROUPS * (part + 1),
+                                    4 * quad : 4 * quad + 4, :].bitcast(I32),
+                )
+            for first in range(STEP_GROUPS * part, STEP_GROUPS * (part + 1), 2):
+                nc.sync.dma_start(
+                    out=win_words[:, first : first + 2, :].bitcast(I32),
+                    in_=words_by_partition(W_in_words)[:, first : first + 2, :],
+                )
+
+        def flip_and_quantise(rows, row_tiles, copiers):
+            pairs = row_tiles // 2
+            grouped = grouped_pool.tile([P, FLIP_BANKS, FLIP_COLS, 4], BF16, tag="grouped", align_bytes=64)
+            codes = operand_pool.tile([P, FLIP_BANKS * FLIP_COLS], U32, tag="codes", align_bytes=64)
+            plane = operand_pool.tile([P, FLIP_BANKS * FLIP_COLS], U8, tag="plane", align_bytes=64)
+            for bank in range(FLIP_BANKS):
+                g, first = bank // pairs, 2 * (bank % pairs)
+                flipped = work_psum.tile([P, 2, FLIP_COLS], F32, tag="work")
+                for u in range(2):
+                    for j in range(2):
+                        words = rows[:, first + j, :].bitcast(F32)
+                        nc.tensor.transpose(
+                            flipped[:, u, P * j : P * (j + 1)],
+                            words[:, WORDS_PASS * g + u : WORDS_PASS * (g + 1) : 2],
+                            ident_f32[:],
+                        )
+                copiers[bank % len(copiers)](
+                    out=grouped[:, bank, :, :].bitcast(F32), in_=flipped[:].rearrange("p u c -> p c u")
+                )
+                if bank % 2 == 1:
+                    both = slice(FLIP_COLS * (bank - 1), FLIP_COLS * (bank + 1))
+                    nc.vector.quantize_mx(
+                        out=codes[:, both].bitcast(FP8X4),
+                        scales=plane[:, both],
+                        in_=grouped[:, bank - 1 : bank + 1, :, :].rearrange("p b c t -> p (b c t)"),
+                    )
+            return codes, plane
+
+        def mx_pass(bank, operand, column, weight_words, weight_plane, start, stop):
+            codes, plane = operand
+            nc.tensor.matmul_mx(
+                out=bank[:],
+                lhsT=codes[:, column : column + P].bitcast(FP8X4),
+                lhsT_scale=plane[:, column : column + P],
+                rhs=weight_words.bitcast(FP8X4),
+                rhs_scale=weight_plane,
+                start=start,
+                stop=stop,
+            )
+
+        x_chunks = {}
+        x_operands = {}
+        xin = {}
+
+        def xin_passes(steps):
+            for j in range(ROUND_TILES):
+                for n_half in range(HALVES):
+                    if steps[0] % STEPS_ROUND == 0:
+                        xin[(j, n_half)] = sum_psum.tile([P, HALF], F32, tag="sum", name="xin_%d_%d" % (j, n_half))
+                    for step in steps:
+                        part = step % STEPS_ROUND
+                        for k in range(STEP_GROUPS):
+                            g = STEP_GROUPS * part + k
+                            mx_pass(
+                                xin[(j, n_half)], x_operands[step], FLIP_COLS * k + P * j,
+                                win_words[:, g, half_cols(n_half)],
+                                win_planes[4 * k : P, part, half_cols(n_half)],
+                                start=(g == 0), stop=(g == GROUPS_IN - 1),
+                            )
+
+        def finish_round(rnd, result_pool):
+            def begin(j, n_half):
+                res = result_pool.tile([P, HALF], F32, tag="res")
+                nc.vector.tensor_tensor(out=res[:], in0=xin[(j, n_half)][:],
+                                        in1=z[:, ROUND_TILES * rnd + j, half_cols(n_half)], op=ALU.add)
+                nc.scalar.activation(out=res[:], in_=res[:], func=ACT.Tanh)
+                return res
+
+            def end(j, n_half, res):
+                i, cols = ROUND_TILES * rnd + j, half_cols(n_half)
+                nc.vector.tensor_tensor(out=res[:], in0=res[:], in1=rate[:, cols], op=ALU.mult)
+                nc.vector.tensor_tensor(out=res[:], in0=res[:], in1=h_rest[:, i, cols], op=ALU.add)
+                nc.sync.dma_start(out=out_rows[:, i, cols], in_=res[:])
+
+            banks = [(j, n_half) for j in range(ROUND_TILES) for n_half in range(HALVES)]
+            begun = begin(*banks[0])
+            for before, bank in zip(banks, banks[1:]):
+                following = begin(*bank)
+                end(*before, begun)
+                begun = following
+            end(*banks[-1], begun)
+
+        with tc.tile_pool(name="hidden", bufs=1) as hidden:
+            liq_sb = hidden.tile([P, ROW_TILES, H], BF16)
+            h_sb = hidden.tile([P, ROW_TILES, H], BF16)
+            v_sb = hidden.tile([P, ROW_TILES, H], BF16)
+            wv_words = hidden.tile([P, GROUPS_H, H], U32, align_bytes=64)
+            wo_words = hidden.tile([P, GROUPS_H, H], U32, align_bytes=64)
+            hid_planes = hidden.tile([P, H], U8, align_bytes=64)
+            vec_rows = hidden.tile([P, H], BF16)
+            bv_all = hidden.tile([P, H], BF16)
+            bo_all = hidden.tile([P, H], BF16)
+            one_minus_rate = hidden.tile([P, H], F32)
+            squares = hidden.tile([P, H], BF16)
+
+            nc.vector.memset(vec_rows[:], 0.0)
+            nc.vector.memset(hid_planes[:].bitcast(I32), 0)
+            nc.vector.memset(win_planes[:].rearrange("p s n -> p (s n)").bitcast(I32), 0)
+            nc.vector.memset(neg_half[:], -0.5)
+            make_identity(nc, ident_f32[:])
+            nc.vector.tensor_copy(out=ident_bf[:], in_=ident_f32[:])
+
+            def load_vector(row, vec):
+                nc.scalar.dma_start(out=vec_rows[row : row + 1, :], in_=vec.rearrange("(o n) -> o n", o=1))
+
+            def load_hidden_weight(words_sb, words, scales, first_partition):
+                for quad in range(4):
+                    rows = slice(32 * quad + first_partition, 32 * quad + first_partition + 4 * GROUPS_H)
+                    nc.sync.dma_start(out=hid_planes[rows, :].bitcast(I32),
+                                      in_=scales[:, 4 * quad : 4 * quad + 4, :].bitcast(I32))
+                nc.sync.dma_start(out=words_sb[:].bitcast(I32), in_=words_by_partition(words))
+
+            load_vector(ROW_BV, b_v)
+            load_vector(ROW_BO, b_o)
+            nc.sync.dma_start(out=liq_sb[:], in_=liq.rearrange("(p i) n -> p i n", i=ROW_TILES))
+            load_hidden_weight(wv_words, W_v_words, W_v_scales, 0)
+            x_chunks[0] = load_x(0)
+            load_vector(ROW_G, g_att)
+            load_vector(ROW_BETA, beta_att)
+            load_vector(ROW_BIN, b_in)
+            load_vector(ROW_TAU, tau)
+            load_win(0)
+            load_hidden_weight(wo_words, W_o_words, W_o_scales, 8)
+            x_chunks[1] = load_x(1)
+            load_win(1)
+            nc.sync.dma_start(out=h_sb[:], in_=h.rearrange("(p i) n -> p i n", i=ROW_TILES))
+            x_chunks[2] = load_x(2)
+            load_win(2)
+
+            def spread(target, vector_rows):
+                for n_half in range(HALVES):
+                    bank = sum_psum.tile([P, HALF], F32, tag="sum")
+                    for count, row in enumerate(vector_rows):
+                        nc.tensor.matmul(
+                            out=bank[:],
+                            lhsT=ident_bf[:, row : row + 1].to_broadcast([P, P]),
+                            rhs=vec_rows[:, half_cols(n_half)],
+                            start=(count == 0),
+                            stop=(count == len(vector_rows) - 1),
+                        )
+                    nc.scalar.copy(out=target[:, half_cols(n_half)], in_=bank[:])
+
+            def project_v(operand):
+                for n_half in range(HALVES):
+                    cols = half_cols(n_half)
+                    for i in range(ROW_TILES):
+                        bank = sum_psum.tile([P, HALF], F32, tag="sum")
+                        for g in range(GROUPS_H):
+                            mx_pass(bank, operand, B * g + P * i, wv_words[:, g, cols],
+                                    hid_planes[4 * g : P, cols], start=(g == 0), stop=(g == GROUPS_H - 1))
+                        nc.vector.tensor_tensor(out=v_sb[:, i, cols], in0=bank[:], in1=bv_all[:, cols], op=ALU.add)
+
+            def attend(i, operand):
+                for n_half in range(HALVES):
+                    cols = half_cols(n_half)
+                    bank = work_psum.tile([P, HALF], F32, tag="work")
+                    for g in range(GROUPS_H):
+                        mx_pass(bank, operand, B * g + P * i, wo_words[:, g, cols],
+                                hid_planes[8 + 4 * g : P, cols], start=(g == 0), stop=(g == GROUPS_H - 1))
+                    nc.vector.scalar_tensor_tensor(
+                        out=z[:, i, cols], in0=bank[:], scalar=1.0, in1=z[:, i, cols],
+                        op0=ALU.mult, op1=ALU.add, accum_out=row_sum[:, i, n_half : n_half + 1],
+                    )
+                nc.vector.tensor_scalar(out=neg_mean[:, i : i + 1], in0=row_sum[:, i, 0:1],
+                                        scalar1=row_sum[:, i, 1:2], scalar2=-1.0 / H, op0=ALU.add, op1=ALU.mult)
+
+            def deviation(i):
+                one = slice(i, i + 1)
+                nc.scalar.activation(out=squares[:], in_=z[:, i, :], func=ACT.Square, bias=neg_mean[:, one],
+                                     scale=1.0, accum_out=sq_sum[:, one])
+                nc.gpsimd.tensor_scalar(out=var_eps[:, one], in0=sq_sum[:, one], scalar1=1.0 / H, scalar2=LN_EPS,
+                                        op0=ALU.mult, op1=ALU.add)
+                nc.gpsimd.tensor_tensor(out=rstd[:, one], in0=var_eps[:, one], in1=neg_half[:], op=ALU.pow)
+
+            def normalise(i):
+                one = slice(i, i + 1)
+                nc.vector.scalar_tensor_tensor(out=z[:, i, :], in0=z[:, i, :], scalar=neg_mean[:, one], in1=gain[:],
+                                               op0=ALU.add, op1=ALU.mult)
+                nc.vector.scalar_tensor_tensor(out=z[:, i, :], in0=z[:, i, :], scalar=rstd[:, one], in1=shift[:],
+                                               op0=ALU.mult, op1=ALU.add)
+
+            def rest_of_h(i):
+                nc.gpsimd.tensor_tensor(out=h_rest[:, i, :], in0=h_sb[:, i, :], in1=one_minus_rate[:], op=ALU.mult)
+
+            spread(bv_all, [ROW_BV])
+            spread(bo_all, [ROW_BO])
+            liq_operand = flip_and_quantise(liq_sb, ROW_TILES, (nc.scalar.copy, nc.vector.tensor_copy))
+            for i in range(ROW_TILES):
+                nc.gpsimd.tensor_tensor(out=z[:, i, :], in0=liq_sb[:, i, :], in1=bo_all[:], op=ALU.add)
+            spread(gain, [ROW_G])
+            spread(shift, [ROW_BETA, ROW_BIN])
+            spread(rate, [ROW_TAU])
+            x_operands[0] = flip_and_quantise(x_chunks[0], ROUND_TILES, (nc.scalar.copy,))
+            x_chunks[3] = load_x(3)
+            load_win(3)
+            project_v(liq_operand)
+            v_operand = flip_and_quantise(v_sb, ROW_TILES, (nc.vector.tensor_copy,))
+            nc.vector.tensor_scalar(out=rate[:], in0=rate[:], scalar1=TAU_EPS, scalar2=None, op0=ALU.add)
+            nc.vector.reciprocal(out=rate[:], in_=rate[:])
+            nc.vector.tensor_scalar(out=one_minus_rate[:], in0=rate[:], scalar1=-1.0, scalar2=1.0,
+                                    op0=ALU.mult, op1=ALU.add)
+            xin_passes((0,))
+            attend(0, v_operand)
+            attend(1, v_operand)
+            x_operands[1] = flip_and_quantise(x_chunks[1], ROUND_TILES, (nc.scalar.copy,))
+            x_chunks[4] = load_x(4)
+            rest_of_h(0)
+            rest_of_h(1)
+            deviation(0)
+            deviation(1)
+            attend(2, v_operand)
+            attend(3, v_operand)
+            normalise(0)
+            normalise(1)
+            x_operands[2] = flip_and_quantise(x_chunks[2], ROUND_TILES, (nc.scalar.copy,))
+            x_chunks[5] = load_x(5)
+            deviation(2)
+            deviation(3)
+            rest_of_h(2)
+            rest_of_h(3)
+            xin_passes((1,))
+            normalise(2)
+            normalise(3)
+
+        with tc.tile_pool(name="results", bufs=4) as results:
+            for step in range(2, STEPS - 2):
+                ahead = step + 1
+                x_operands[ahead] = flip_and_quantise(x_chunks[ahead], ROUND_TILES, (nc.scalar.copy,))
+                if ahead + X_AHEAD < STEPS:
+                    x_chunks[ahead + X_AHEAD] = load_x(ahead + X_AHEAD)
+                xin_passes((step,))
+                if step == STEPS_ROUND - 1:
+                    finish_round(0, results)
+            x_operands[STEPS - 1] = flip_and_quantise(x_chunks[STEPS - 1], ROUND_TILES, (nc.scalar.copy,))
+            xin_passes((STEPS - 2, STEPS - 1))
+            finish_round(1, results)

@@ -59,8 +59,7 @@ def tile_advancedliquidneuralnetwork_pb_k_kernel(
         x_pool = stack.enter_context(tc.tile_pool(name="x_pool", bufs=X_AHEAD))
         grouped_pool = stack.enter_context(tc.tile_pool(name="grouped_pool", bufs=2))
         operand_pool = stack.enter_context(tc.tile_pool(name="operand_pool", bufs=4))
-        sum_psum = stack.enter_context(tc.psum_pool(name="sum_psum", bufs=4))
-        work_psum = stack.enter_context(tc.psum_pool(name="work_psum", bufs=4))
+        psum = stack.enter_context(tc.psum_pool(name="psum", bufs=4))
 
         win_words = keep.tile([P, GROUPS_IN, H], U32, align_bytes=64)
         win_planes = keep.tile([P, STEPS_ROUND, H], U8, align_bytes=64)
@@ -78,15 +77,19 @@ def tile_advancedliquidneuralnetwork_pb_k_kernel(
         rstd = keep.tile([P, ROW_TILES], F32)
         neg_half = keep.tile([P, 1], F32)
 
+        x_chunks = {}
+        x_operands = {}
+        xin = {}
+
         def load_x(step):
             rnd, part = divmod(step, STEPS_ROUND)
-            chunk = x_pool.tile([P, ROUND_TILES, STEP_GROUPS * K_PASS], BF16, tag="x_chunk")
+            x_chunks[step] = x_pool.tile([P, ROUND_TILES, STEP_GROUPS * K_PASS], BF16, tag="x_chunk",
+                                         name="x_chunk_%d" % step)
             nc.sync.dma_start(
-                out=chunk[:],
+                out=x_chunks[step][:],
                 in_=x_rows[:, ROUND_TILES * rnd : ROUND_TILES * (rnd + 1),
                            STEP_GROUPS * K_PASS * part : STEP_GROUPS * K_PASS * (part + 1)],
             )
-            return chunk
 
         def load_win(part):
             for quad in range(4):
@@ -108,7 +111,7 @@ def tile_advancedliquidneuralnetwork_pb_k_kernel(
             plane = operand_pool.tile([P, FLIP_BANKS * FLIP_COLS], U8, tag="plane", align_bytes=64)
             for bank in range(FLIP_BANKS):
                 g, first = bank // pairs, 2 * (bank % pairs)
-                flipped = work_psum.tile([P, 2, FLIP_COLS], F32, tag="work")
+                flipped = psum.tile([P, 2, FLIP_COLS], F32, tag="work")
                 for u in range(2):
                     for j in range(2):
                         words = rows[:, first + j, :].bitcast(F32)
@@ -129,6 +132,11 @@ def tile_advancedliquidneuralnetwork_pb_k_kernel(
                     )
             return codes, plane
 
+        def flip_x(step):
+            x_operands[step] = flip_and_quantise(x_chunks[step], ROUND_TILES, (nc.scalar.copy,))
+            if step + X_AHEAD < STEPS:
+                load_x(step + X_AHEAD)
+
         def mx_pass(bank, operand, column, weight_words, weight_plane, start, stop):
             codes, plane = operand
             nc.tensor.matmul_mx(
@@ -141,15 +149,11 @@ def tile_advancedliquidneuralnetwork_pb_k_kernel(
                 stop=stop,
             )
 
-        x_chunks = {}
-        x_operands = {}
-        xin = {}
-
         def xin_passes(steps):
             for j in range(ROUND_TILES):
                 for n_half in range(HALVES):
                     if steps[0] % STEPS_ROUND == 0:
-                        xin[(j, n_half)] = sum_psum.tile([P, HALF], F32, tag="sum", name="xin_%d_%d" % (j, n_half))
+                        xin[(j, n_half)] = psum.tile([P, HALF], F32, tag="sum", name="xin_%d_%d" % (j, n_half))
                     for step in steps:
                         part = step % STEPS_ROUND
                         for k in range(STEP_GROUPS):
@@ -160,6 +164,13 @@ def tile_advancedliquidneuralnetwork_pb_k_kernel(
                                 win_planes[4 * k : P, part, half_cols(n_half)],
                                 start=(g == 0), stop=(g == GROUPS_IN - 1),
                             )
+
+        def normalise(i):
+            one = slice(i, i + 1)
+            nc.vector.scalar_tensor_tensor(out=z[:, i, :], in0=z[:, i, :], scalar=neg_mean[:, one], in1=gain[:],
+                                           op0=ALU.add, op1=ALU.mult)
+            nc.vector.scalar_tensor_tensor(out=z[:, i, :], in0=z[:, i, :], scalar=rstd[:, one], in1=shift[:],
+                                           op0=ALU.mult, op1=ALU.add)
 
         def finish_round(rnd, result_pool):
             def begin(j, n_half):
@@ -203,9 +214,6 @@ def tile_advancedliquidneuralnetwork_pb_k_kernel(
             make_identity(nc, ident_f32[:])
             nc.vector.tensor_copy(out=ident_bf[:], in_=ident_f32[:])
 
-            def load_vector(row, vec):
-                nc.scalar.dma_start(out=vec_rows[row : row + 1, :], in_=vec.rearrange("(o n) -> o n", o=1))
-
             def load_hidden_weight(words_sb, words, scales, first_partition):
                 for quad in range(4):
                     rows = slice(32 * quad + first_partition, 32 * quad + first_partition + 4 * GROUPS_H)
@@ -213,26 +221,21 @@ def tile_advancedliquidneuralnetwork_pb_k_kernel(
                                       in_=scales[:, 4 * quad : 4 * quad + 4, :].bitcast(I32))
                 nc.sync.dma_start(out=words_sb[:].bitcast(I32), in_=words_by_partition(words))
 
-            load_vector(ROW_BV, b_v)
-            load_vector(ROW_BO, b_o)
+            for row, vec in ((ROW_BV, b_v), (ROW_BO, b_o), (ROW_G, g_att), (ROW_BETA, beta_att),
+                             (ROW_BIN, b_in), (ROW_TAU, tau)):
+                nc.scalar.dma_start(out=vec_rows[row : row + 1, :], in_=vec.rearrange("(o n) -> o n", o=1))
             nc.sync.dma_start(out=liq_sb[:], in_=liq.rearrange("(p i) n -> p i n", i=ROW_TILES))
             load_hidden_weight(wv_words, W_v_words, W_v_scales, 0)
-            x_chunks[0] = load_x(0)
-            load_vector(ROW_G, g_att)
-            load_vector(ROW_BETA, beta_att)
-            load_vector(ROW_BIN, b_in)
-            load_vector(ROW_TAU, tau)
+            load_x(0)
             load_win(0)
             load_hidden_weight(wo_words, W_o_words, W_o_scales, 8)
-            x_chunks[1] = load_x(1)
+            load_x(1)
+            load_x(2)
             load_win(1)
-            nc.sync.dma_start(out=h_sb[:], in_=h.rearrange("(p i) n -> p i n", i=ROW_TILES))
-            x_chunks[2] = load_x(2)
-            load_win(2)
 
             def spread(target, vector_rows):
-                for n_half in range(HALVES):
-                    bank = sum_psum.tile([P, HALF], F32, tag="sum")
+                for n_half, copy_out in enumerate((nc.scalar.copy, nc.vector.tensor_copy)):
+                    bank = psum.tile([P, HALF], F32, tag="sum")
                     for count, row in enumerate(vector_rows):
                         nc.tensor.matmul(
                             out=bank[:],
@@ -241,22 +244,21 @@ def tile_advancedliquidneuralnetwork_pb_k_kernel(
                             start=(count == 0),
                             stop=(count == len(vector_rows) - 1),
                         )
-                    nc.scalar.copy(out=target[:, half_cols(n_half)], in_=bank[:])
+                    copy_out(out=target[:, half_cols(n_half)], in_=bank[:])
 
-            def project_v(operand):
-                for n_half in range(HALVES):
-                    cols = half_cols(n_half)
-                    for i in range(ROW_TILES):
-                        bank = sum_psum.tile([P, HALF], F32, tag="sum")
-                        for g in range(GROUPS_H):
-                            mx_pass(bank, operand, B * g + P * i, wv_words[:, g, cols],
-                                    hid_planes[4 * g : P, cols], start=(g == 0), stop=(g == GROUPS_H - 1))
-                        nc.vector.tensor_tensor(out=v_sb[:, i, cols], in0=bank[:], in1=bv_all[:, cols], op=ALU.add)
+            def project_v(operand, n_half, tag):
+                cols = half_cols(n_half)
+                for i in range(ROW_TILES):
+                    bank = psum.tile([P, HALF], F32, tag=tag)
+                    for g in range(GROUPS_H):
+                        mx_pass(bank, operand, B * g + P * i, wv_words[:, g, cols],
+                                hid_planes[4 * g : P, cols], start=(g == 0), stop=(g == GROUPS_H - 1))
+                    nc.vector.tensor_tensor(out=v_sb[:, i, cols], in0=bank[:], in1=bv_all[:, cols], op=ALU.add)
 
             def attend(i, operand):
                 for n_half in range(HALVES):
                     cols = half_cols(n_half)
-                    bank = work_psum.tile([P, HALF], F32, tag="work")
+                    bank = psum.tile([P, HALF], F32, tag="work")
                     for g in range(GROUPS_H):
                         mx_pass(bank, operand, B * g + P * i, wo_words[:, g, cols],
                                 hid_planes[8 + 4 * g : P, cols], start=(g == 0), stop=(g == GROUPS_H - 1))
@@ -275,28 +277,18 @@ def tile_advancedliquidneuralnetwork_pb_k_kernel(
                                         op0=ALU.mult, op1=ALU.add)
                 nc.gpsimd.tensor_tensor(out=rstd[:, one], in0=var_eps[:, one], in1=neg_half[:], op=ALU.pow)
 
-            def normalise(i):
-                one = slice(i, i + 1)
-                nc.vector.scalar_tensor_tensor(out=z[:, i, :], in0=z[:, i, :], scalar=neg_mean[:, one], in1=gain[:],
-                                               op0=ALU.add, op1=ALU.mult)
-                nc.vector.scalar_tensor_tensor(out=z[:, i, :], in0=z[:, i, :], scalar=rstd[:, one], in1=shift[:],
-                                               op0=ALU.mult, op1=ALU.add)
-
-            def rest_of_h(i):
-                nc.gpsimd.tensor_tensor(out=h_rest[:, i, :], in0=h_sb[:, i, :], in1=one_minus_rate[:], op=ALU.mult)
-
             spread(bv_all, [ROW_BV])
-            spread(bo_all, [ROW_BO])
-            liq_operand = flip_and_quantise(liq_sb, ROW_TILES, (nc.scalar.copy, nc.vector.tensor_copy))
-            for i in range(ROW_TILES):
-                nc.gpsimd.tensor_tensor(out=z[:, i, :], in0=liq_sb[:, i, :], in1=bo_all[:], op=ALU.add)
             spread(gain, [ROW_G])
+            liq_operand = flip_and_quantise(liq_sb, ROW_TILES, (nc.scalar.copy, nc.vector.tensor_copy))
             spread(shift, [ROW_BETA, ROW_BIN])
             spread(rate, [ROW_TAU])
-            x_operands[0] = flip_and_quantise(x_chunks[0], ROUND_TILES, (nc.scalar.copy,))
-            x_chunks[3] = load_x(3)
-            load_win(3)
-            project_v(liq_operand)
+            spread(bo_all, [ROW_BO])
+            project_v(liq_operand, 0, "work")
+            project_v(liq_operand, 1, "sum")
+            for i in range(ROW_TILES):
+                nc.gpsimd.tensor_tensor(out=z[:, i, :], in0=liq_sb[:, i, :], in1=bo_all[:], op=ALU.add)
+            flip_x(0)
+            load_win(2)
             v_operand = flip_and_quantise(v_sb, ROW_TILES, (nc.vector.tensor_copy,))
             nc.vector.tensor_scalar(out=rate[:], in0=rate[:], scalar1=TAU_EPS, scalar2=None, op0=ALU.add)
             nc.vector.reciprocal(out=rate[:], in_=rate[:])
@@ -305,35 +297,34 @@ def tile_advancedliquidneuralnetwork_pb_k_kernel(
             xin_passes((0,))
             attend(0, v_operand)
             attend(1, v_operand)
-            x_operands[1] = flip_and_quantise(x_chunks[1], ROUND_TILES, (nc.scalar.copy,))
-            x_chunks[4] = load_x(4)
-            rest_of_h(0)
-            rest_of_h(1)
+            flip_x(1)
+            load_win(3)
+            nc.sync.dma_start(out=h_sb[:], in_=h.rearrange("(p i) n -> p i n", i=ROW_TILES))
             deviation(0)
             deviation(1)
             attend(2, v_operand)
             attend(3, v_operand)
-            normalise(0)
-            normalise(1)
-            x_operands[2] = flip_and_quantise(x_chunks[2], ROUND_TILES, (nc.scalar.copy,))
-            x_chunks[5] = load_x(5)
+            flip_x(2)
             deviation(2)
             deviation(3)
-            rest_of_h(2)
-            rest_of_h(3)
+            normalise(0)
             xin_passes((1,))
-            normalise(2)
-            normalise(3)
+            normalise(1)
+            flip_x(3)
+            xin_passes((2,))
+            for i in range(ROW_TILES):
+                nc.gpsimd.tensor_tensor(out=h_rest[:, i, :], in0=h_sb[:, i, :], in1=one_minus_rate[:], op=ALU.mult)
 
-        with tc.tile_pool(name="results", bufs=4) as results:
-            for step in range(2, STEPS - 2):
-                ahead = step + 1
-                x_operands[ahead] = flip_and_quantise(x_chunks[ahead], ROUND_TILES, (nc.scalar.copy,))
-                if ahead + X_AHEAD < STEPS:
-                    x_chunks[ahead + X_AHEAD] = load_x(ahead + X_AHEAD)
-                xin_passes((step,))
-                if step == STEPS_ROUND - 1:
-                    finish_round(0, results)
-            x_operands[STEPS - 1] = flip_and_quantise(x_chunks[STEPS - 1], ROUND_TILES, (nc.scalar.copy,))
-            xin_passes((STEPS - 2, STEPS - 1))
+        with tc.tile_pool(name="results", bufs=4, reuse_waits="tile") as results:
+            flip_x(4)
+            xin_passes((3,))
+            finish_round(0, results)
+            flip_x(5)
+            xin_passes((4,))
+            normalise(2)
+            flip_x(6)
+            xin_passes((5,))
+            normalise(3)
+            flip_x(7)
+            xin_passes((6, 7))
             finish_round(1, results)

@@ -200,7 +200,8 @@ def tile_advancedliquidneuralnetwork_pb_k_kernel(
             v_sb = hidden.tile([P, ROW_TILES, H], BF16)
             wv_words = hidden.tile([P, GROUPS_H, H], U32, align_bytes=64)
             wo_words = hidden.tile([P, GROUPS_H, H], U32, align_bytes=64)
-            hid_planes = hidden.tile([P, H], U8, align_bytes=64)
+            wv_planes = hidden.tile([P, H], U8, align_bytes=64)
+            wo_planes = hidden.tile([P, H], U8, align_bytes=64)
             vec_rows = hidden.tile([P, H], BF16)
             bv_all = hidden.tile([P, H], BF16)
             bo_all = hidden.tile([P, H], BF16)
@@ -208,27 +209,30 @@ def tile_advancedliquidneuralnetwork_pb_k_kernel(
             squares = hidden.tile([P, H], BF16)
 
             nc.vector.memset(vec_rows[:], 0.0)
-            nc.vector.memset(hid_planes[:].bitcast(I32), 0)
+            nc.vector.memset(wv_planes[:].bitcast(I32), 0)
+            nc.vector.memset(wo_planes[:].bitcast(I32), 0)
             nc.vector.memset(win_planes[:].rearrange("p s n -> p (s n)").bitcast(I32), 0)
             nc.vector.memset(neg_half[:], -0.5)
             make_identity(nc, ident_f32[:])
             nc.vector.tensor_copy(out=ident_bf[:], in_=ident_f32[:])
 
-            def load_hidden_weight(words_sb, words, scales, first_partition):
+            def load_hidden_weight(words_sb, planes_sb, words, scales):
                 for quad in range(4):
-                    rows = slice(32 * quad + first_partition, 32 * quad + first_partition + 4 * GROUPS_H)
-                    nc.sync.dma_start(out=hid_planes[rows, :].bitcast(I32),
+                    nc.sync.dma_start(out=planes_sb[32 * quad : 32 * quad + 4 * GROUPS_H, :].bitcast(I32),
                                       in_=scales[:, 4 * quad : 4 * quad + 4, :].bitcast(I32))
                 nc.sync.dma_start(out=words_sb[:].bitcast(I32), in_=words_by_partition(words))
 
             for row, vec in ((ROW_BV, b_v), (ROW_BO, b_o), (ROW_G, g_att), (ROW_BETA, beta_att),
                              (ROW_BIN, b_in), (ROW_TAU, tau)):
-                nc.scalar.dma_start(out=vec_rows[row : row + 1, :], in_=vec.rearrange("(o n) -> o n", o=1))
-            nc.sync.dma_start(out=liq_sb[:], in_=liq.rearrange("(p i) n -> p i n", i=ROW_TILES))
-            load_hidden_weight(wv_words, W_v_words, W_v_scales, 0)
+                nc.sync.dma_start(out=vec_rows[row : row + 1, :], in_=vec.rearrange("(o n) -> o n", o=1))
+            liq_rows = liq.rearrange("(p i) n -> p i n", i=ROW_TILES)
+            for g in range(GROUPS_H):
+                nc.sync.dma_start(out=liq_sb[:, :, K_PASS * g : K_PASS * (g + 1)],
+                                  in_=liq_rows[:, :, K_PASS * g : K_PASS * (g + 1)])
+            load_hidden_weight(wv_words, wv_planes, W_v_words, W_v_scales)
             load_x(0)
             load_win(0)
-            load_hidden_weight(wo_words, W_o_words, W_o_scales, 8)
+            load_hidden_weight(wo_words, wo_planes, W_o_words, W_o_scales)
             load_x(1)
             load_x(2)
             load_win(1)
@@ -252,7 +256,7 @@ def tile_advancedliquidneuralnetwork_pb_k_kernel(
                     bank = psum.tile([P, HALF], F32, tag=tag)
                     for g in range(GROUPS_H):
                         mx_pass(bank, operand, B * g + P * i, wv_words[:, g, cols],
-                                hid_planes[4 * g : P, cols], start=(g == 0), stop=(g == GROUPS_H - 1))
+                                wv_planes[4 * g : P, cols], start=(g == 0), stop=(g == GROUPS_H - 1))
                     nc.vector.tensor_tensor(out=v_sb[:, i, cols], in0=bank[:], in1=bv_all[:, cols], op=ALU.add)
 
             def attend(i, operand):
@@ -261,7 +265,7 @@ def tile_advancedliquidneuralnetwork_pb_k_kernel(
                     bank = psum.tile([P, HALF], F32, tag="work")
                     for g in range(GROUPS_H):
                         mx_pass(bank, operand, B * g + P * i, wo_words[:, g, cols],
-                                hid_planes[8 + 4 * g : P, cols], start=(g == 0), stop=(g == GROUPS_H - 1))
+                                wo_planes[4 * g : P, cols], start=(g == 0), stop=(g == GROUPS_H - 1))
                     nc.vector.scalar_tensor_tensor(
                         out=z[:, i, cols], in0=bank[:], scalar=1.0, in1=z[:, i, cols],
                         op0=ALU.mult, op1=ALU.add, accum_out=row_sum[:, i, n_half : n_half + 1],
@@ -278,11 +282,11 @@ def tile_advancedliquidneuralnetwork_pb_k_kernel(
                 nc.gpsimd.tensor_tensor(out=rstd[:, one], in0=var_eps[:, one], in1=neg_half[:], op=ALU.pow)
 
             spread(bv_all, [ROW_BV])
-            spread(gain, [ROW_G])
-            liq_operand = flip_and_quantise(liq_sb, ROW_TILES, (nc.scalar.copy, nc.vector.tensor_copy))
-            spread(shift, [ROW_BETA, ROW_BIN])
-            spread(rate, [ROW_TAU])
             spread(bo_all, [ROW_BO])
+            liq_operand = flip_and_quantise(liq_sb, ROW_TILES, (nc.scalar.copy, nc.vector.tensor_copy))
+            spread(rate, [ROW_TAU])
+            spread(gain, [ROW_G])
+            spread(shift, [ROW_BETA, ROW_BIN])
             project_v(liq_operand, 0, "work")
             project_v(liq_operand, 1, "sum")
             for i in range(ROW_TILES):

@@ -237,8 +237,8 @@ def tile_advancedliquidneuralnetwork_pb_k_kernel(
             load_x(2)
             load_win(1)
 
-            def spread(target, vector_rows):
-                for n_half, copy_out in enumerate((nc.scalar.copy, nc.vector.tensor_copy)):
+            def spread(target, vector_rows, plus=0.0):
+                for n_half in range(HALVES):
                     bank = psum.tile([P, HALF], F32, tag="sum")
                     for count, row in enumerate(vector_rows):
                         nc.tensor.matmul(
@@ -248,7 +248,7 @@ def tile_advancedliquidneuralnetwork_pb_k_kernel(
                             start=(count == 0),
                             stop=(count == len(vector_rows) - 1),
                         )
-                    copy_out(out=target[:, half_cols(n_half)], in_=bank[:])
+                    nc.scalar.activation(out=target[:, half_cols(n_half)], in_=bank[:], func=ACT.Copy, bias=plus, scale=1.0)
 
             def project_v(operand, n_half, tag):
                 cols = half_cols(n_half)
@@ -284,7 +284,7 @@ def tile_advancedliquidneuralnetwork_pb_k_kernel(
             spread(bv_all, [ROW_BV])
             spread(bo_all, [ROW_BO])
             liq_operand = flip_and_quantise(liq_sb, ROW_TILES, (nc.scalar.copy, nc.vector.tensor_copy))
-            spread(rate, [ROW_TAU])
+            spread(rate, [ROW_TAU], plus=TAU_EPS)
             spread(gain, [ROW_G])
             spread(shift, [ROW_BETA, ROW_BIN])
             project_v(liq_operand, 0, "work")
@@ -293,28 +293,26 @@ def tile_advancedliquidneuralnetwork_pb_k_kernel(
                 nc.gpsimd.tensor_tensor(out=z[:, i, :], in0=liq_sb[:, i, :], in1=bo_all[:], op=ALU.add)
             flip_x(0)
             load_win(2)
-            v_operand = flip_and_quantise(v_sb, ROW_TILES, (nc.vector.tensor_copy,))
-            nc.vector.tensor_scalar(out=rate[:], in0=rate[:], scalar1=TAU_EPS, scalar2=None, op0=ALU.add)
-            nc.vector.reciprocal(out=rate[:], in_=rate[:])
-            nc.vector.tensor_scalar(out=one_minus_rate[:], in0=rate[:], scalar1=-1.0, scalar2=1.0,
-                                    op0=ALU.mult, op1=ALU.add)
+            v_operand = flip_and_quantise(v_sb, ROW_TILES, (nc.scalar.copy, nc.vector.tensor_copy))
             xin_passes((0,))
-            attend(0, v_operand)
-            attend(1, v_operand)
             flip_x(1)
             load_win(3)
             nc.sync.dma_start(out=h_sb[:], in_=h.rearrange("(p i) n -> p i n", i=ROW_TILES))
+            attend(0, v_operand)
+            attend(1, v_operand)
+            flip_x(2)
             deviation(0)
             deviation(1)
+            nc.vector.reciprocal(out=rate[:], in_=rate[:])
+            nc.scalar.activation(out=one_minus_rate[:], in_=rate[:], func=ACT.Copy, bias=1.0, scale=-1.0)
+            xin_passes((1,))
             attend(2, v_operand)
             attend(3, v_operand)
-            flip_x(2)
+            normalise(0)
+            flip_x(3)
             deviation(2)
             deviation(3)
-            normalise(0)
-            xin_passes((1,))
             normalise(1)
-            flip_x(3)
             xin_passes((2,))
             for i in range(ROW_TILES):
                 nc.gpsimd.tensor_tensor(out=h_rest[:, i, :], in0=h_sb[:, i, :], in1=one_minus_rate[:], op=ALU.mult)

@@ -60,6 +60,7 @@ def tile_advancedliquidneuralnetwork_pb_k_kernel(
         grouped_pool = stack.enter_context(tc.tile_pool(name="grouped_pool", bufs=2))
         operand_pool = stack.enter_context(tc.tile_pool(name="operand_pool", bufs=4))
         psum = stack.enter_context(tc.psum_pool(name="psum", bufs=4))
+        results = stack.enter_context(tc.tile_pool(name="results", bufs=4))
 
         win_words = keep.tile([P, GROUPS_IN, H], U32, align_bytes=64)
         win_planes = keep.tile([P, STEPS_ROUND, H], U8, align_bytes=64)
@@ -281,6 +282,9 @@ def tile_advancedliquidneuralnetwork_pb_k_kernel(
                                         op0=ALU.mult, op1=ALU.add)
                 nc.gpsimd.tensor_tensor(out=rstd[:, one], in0=var_eps[:, one], in1=neg_half[:], op=ALU.pow)
 
+            def rest_of_h(i):
+                nc.vector.tensor_tensor(out=h_rest[:, i, :], in0=h_sb[:, i, :], in1=one_minus_rate[:], op=ALU.mult)
+
             spread(bv_all, [ROW_BV])
             spread(bo_all, [ROW_BO])
             liq_operand = flip_and_quantise(liq_sb, ROW_TILES, (nc.scalar.copy, nc.vector.tensor_copy))
@@ -289,11 +293,11 @@ def tile_advancedliquidneuralnetwork_pb_k_kernel(
             spread(shift, [ROW_BETA, ROW_BIN])
             project_v(liq_operand, 0, "work")
             project_v(liq_operand, 1, "sum")
-            for i in range(ROW_TILES):
-                nc.gpsimd.tensor_tensor(out=z[:, i, :], in0=liq_sb[:, i, :], in1=bo_all[:], op=ALU.add)
             flip_x(0)
             load_win(2)
             v_operand = flip_and_quantise(v_sb, ROW_TILES, (nc.scalar.copy, nc.vector.tensor_copy))
+            for i in range(ROW_TILES):
+                nc.vector.tensor_tensor(out=z[:, i, :], in0=liq_sb[:, i, :], in1=bo_all[:], op=ALU.add)
             xin_passes((0,))
             flip_x(1)
             load_win(3)
@@ -314,19 +318,20 @@ def tile_advancedliquidneuralnetwork_pb_k_kernel(
             deviation(3)
             normalise(1)
             xin_passes((2,))
-            for i in range(ROW_TILES):
-                nc.gpsimd.tensor_tensor(out=h_rest[:, i, :], in0=h_sb[:, i, :], in1=one_minus_rate[:], op=ALU.mult)
+            rest_of_h(0)
+            rest_of_h(1)
 
-        with tc.tile_pool(name="results", bufs=4, reuse_waits="tile") as results:
             flip_x(4)
             xin_passes((3,))
             finish_round(0, results)
             flip_x(5)
             xin_passes((4,))
             normalise(2)
+            rest_of_h(2)
             flip_x(6)
             xin_passes((5,))
             normalise(3)
+            rest_of_h(3)
             flip_x(7)
             xin_passes((6, 7))
             finish_round(1, results)

@@ -21,20 +21,20 @@ K_PASS = 4 * P
 WORDS_PASS = K_PASS // 2
 HALF = 512
 HALVES = H // HALF
+QUARTER = HALF // 2
 GROUPS_H = H // K_PASS
 GROUPS_IN = IN // K_PASS
-ROUND_TILES = 2
-ROUNDS = ROW_TILES // ROUND_TILES
-STEP_GROUPS = 4
-STEPS_ROUND = GROUPS_IN // STEP_GROUPS
-STEPS = ROUNDS * STEPS_ROUND
-FLIP_BANKS = 4
-FLIP_COLS = 2 * P
-X_AHEAD = 3
+CHUNK = 2
+CHUNKS = GROUPS_IN // CHUNK
+PLANE_GROUPS = 4
+PLANE_SETS = GROUPS_IN // PLANE_GROUPS
+ROW_BUFFERS = 4
+WARM_UP = 8
+TAU_COLS = H // P
 
 FLOPS = 2 * B * H * (IN + H + H)
 
-ROW_BV, ROW_BO, ROW_G, ROW_BETA, ROW_BIN, ROW_TAU = 0, 1, 2, 3, 4, 5
+ROW_BO, ROW_G, ROW_BETA, ROW_BIN = 0, 1, 2, 3
 
 
 def half_cols(n_half):
@@ -51,24 +51,37 @@ def tile_advancedliquidneuralnetwork_pb_k_kernel(
 ):
     nc = tc.nc
     x_rows = x.rearrange("(p i) k -> p i k", i=ROW_TILES)
+    liq_rows = liq.rearrange("(p i) n -> p i n", i=ROW_TILES)
+    h_rows = h.rearrange("(p i) n -> p i n", i=ROW_TILES)
     out_rows = out.rearrange("(p i) n -> p i n", i=ROW_TILES)
 
     with ExitStack() as stack:
         stack.enter_context(tc.manual_schedule())
         keep = stack.enter_context(tc.tile_pool(name="keep", bufs=1))
-        x_pool = stack.enter_context(tc.tile_pool(name="x_pool", bufs=X_AHEAD))
-        grouped_pool = stack.enter_context(tc.tile_pool(name="grouped_pool", bufs=2))
-        operand_pool = stack.enter_context(tc.tile_pool(name="operand_pool", bufs=4))
+        rows_pool = stack.enter_context(tc.tile_pool(name="rows_pool", bufs=ROW_BUFFERS))
+        grouped_pool = stack.enter_context(tc.tile_pool(name="grouped_pool", bufs=3))
+        operand_pool = stack.enter_context(tc.tile_pool(name="operand_pool", bufs=GROUPS_IN))
         psum = stack.enter_context(tc.psum_pool(name="psum", bufs=4))
         results = stack.enter_context(tc.tile_pool(name="results", bufs=4))
 
         win_words = keep.tile([P, GROUPS_IN, H], U32, align_bytes=64)
-        win_planes = keep.tile([P, STEPS_ROUND, H], U8, align_bytes=64)
+        win_planes = keep.tile([P, PLANE_SETS, H], U8, align_bytes=64)
+        wo_words = keep.tile([P, GROUPS_H, H], U32, align_bytes=64)
+        wv_planes = keep.tile([P, H], U8, align_bytes=64)
+        wo_planes = keep.tile([P, H], U8, align_bytes=64)
+        wv_words_ctm = keep.tile([P, GROUPS_H, H], U32, align_bytes=64)
+        wv_planes_ctm = keep.tile([P, H], U8, align_bytes=64)
         ident_f32 = keep.tile([P, P], F32)
         ident_bf = keep.tile([P, P], BF16)
+        vec_rows = keep.tile([P, H], BF16)
+        bv_sb = keep.tile([P, GROUPS_H, 4], BF16)
+        tau_sb = keep.tile([P, TAU_COLS], BF16)
+        rate_cols = keep.tile([P, TAU_COLS], F32)
+        bo_all = keep.tile([P, H], BF16)
         gain = keep.tile([P, H], BF16)
         shift = keep.tile([P, H], F32)
         rate = keep.tile([P, H], F32)
+        one_minus_rate = keep.tile([P, H], F32)
         z = keep.tile([P, ROW_TILES, H], F32)
         h_rest = keep.tile([P, ROW_TILES, H], F32)
         row_sum = keep.tile([P, ROW_TILES, HALVES], F32)
@@ -78,260 +91,298 @@ def tile_advancedliquidneuralnetwork_pb_k_kernel(
         rstd = keep.tile([P, ROW_TILES], F32)
         neg_half = keep.tile([P, 1], F32)
 
-        x_chunks = {}
-        x_operands = {}
-        xin = {}
-
-        def load_x(step):
-            rnd, part = divmod(step, STEPS_ROUND)
-            x_chunks[step] = x_pool.tile([P, ROUND_TILES, STEP_GROUPS * K_PASS], BF16, tag="x_chunk",
-                                         name="x_chunk_%d" % step)
-            nc.sync.dma_start(
-                out=x_chunks[step][:],
-                in_=x_rows[:, ROUND_TILES * rnd : ROUND_TILES * (rnd + 1),
-                           STEP_GROUPS * K_PASS * part : STEP_GROUPS * K_PASS * (part + 1)],
-            )
-
-        def load_win(part):
+        def load_planes(planes, scales):
+            groups = scales.shape[0]
             for quad in range(4):
-                nc.sync.dma_start(
-                    out=win_planes[32 * quad : 32 * quad + 16, part, :].bitcast(I32),
-                    in_=W_in_scales[STEP_GROUPS * part : STEP_GROUPS * (part + 1),
-                                    4 * quad : 4 * quad + 4, :].bitcast(I32),
-                )
-            for first in range(STEP_GROUPS * part, STEP_GROUPS * (part + 1), 2):
-                nc.sync.dma_start(
-                    out=win_words[:, first : first + 2, :].bitcast(I32),
-                    in_=words_by_partition(W_in_words)[:, first : first + 2, :],
-                )
+                nc.sync.dma_start(out=planes[32 * quad : 32 * quad + 4 * groups, :].bitcast(I32),
+                                  in_=scales[:, 4 * quad : 4 * quad + 4, :].bitcast(I32))
 
-        def flip_and_quantise(rows, row_tiles, copiers):
-            pairs = row_tiles // 2
-            grouped = grouped_pool.tile([P, FLIP_BANKS, FLIP_COLS, 4], BF16, tag="grouped", align_bytes=64)
-            codes = operand_pool.tile([P, FLIP_BANKS * FLIP_COLS], U32, tag="codes", align_bytes=64)
-            plane = operand_pool.tile([P, FLIP_BANKS * FLIP_COLS], U8, tag="plane", align_bytes=64)
-            for bank in range(FLIP_BANKS):
-                g, first = bank // pairs, 2 * (bank % pairs)
-                flipped = psum.tile([P, 2, FLIP_COLS], F32, tag="work")
-                for u in range(2):
-                    for j in range(2):
-                        words = rows[:, first + j, :].bitcast(F32)
-                        nc.tensor.transpose(
-                            flipped[:, u, P * j : P * (j + 1)],
-                            words[:, WORDS_PASS * g + u : WORDS_PASS * (g + 1) : 2],
-                            ident_f32[:],
-                        )
-                copiers[bank % len(copiers)](
-                    out=grouped[:, bank, :, :].bitcast(F32), in_=flipped[:].rearrange("p u c -> p c u")
-                )
-                if bank % 2 == 1:
-                    both = slice(FLIP_COLS * (bank - 1), FLIP_COLS * (bank + 1))
-                    nc.vector.quantize_mx(
-                        out=codes[:, both].bitcast(FP8X4),
-                        scales=plane[:, both],
-                        in_=grouped[:, bank - 1 : bank + 1, :, :].rearrange("p b c t -> p (b c t)"),
+        def load_win_planes(which):
+            load_planes(win_planes[:, which, :], W_in_scales[PLANE_GROUPS * which : PLANE_GROUPS * (which + 1)])
+
+        def load_win(chunk, n_half):
+            groups = slice(CHUNK * chunk, CHUNK * (chunk + 1))
+            nc.sync.dma_start(out=win_words[:, groups, half_cols(n_half)].bitcast(I32),
+                              in_=words_by_partition(W_in_words)[:, groups, half_cols(n_half)])
+
+        def new_rows(name):
+            return rows_pool.tile([P, ROW_TILES, H], BF16, tag="rows", align_bytes=64, name=name)
+
+        def load_x(chunk):
+            rows = new_rows("x_%d" % chunk)
+            nc.sync.dma_start(out=rows[:], in_=x_rows[:, :, H * chunk : H * (chunk + 1)])
+            return rows
+
+        def spread(target, vector_rows):
+            for n_half in range(HALVES):
+                bank = psum.tile([P, HALF], F32, tag="sum")
+                for count, row in enumerate(vector_rows):
+                    nc.tensor.matmul(
+                        out=bank[:],
+                        lhsT=ident_bf[:, row : row + 1].to_broadcast([P, P]),
+                        rhs=vec_rows[:, half_cols(n_half)],
+                        start=(count == 0),
+                        stop=(count == len(vector_rows) - 1),
                     )
+                nc.scalar.copy(out=target[:, half_cols(n_half)], in_=bank[:])
+
+        def spread_rate():
+            rate_by_col = rate[:].rearrange("p (q m) -> p q m", m=TAU_COLS)
+            in_bank = TAU_COLS // 2
+            for part in range(2):
+                bank = psum.tile([P, in_bank, P], F32, tag="sum")
+                for m in range(in_bank):
+                    col = in_bank * part + m
+                    nc.tensor.transpose(bank[:, m, :], rate_cols[:, col : col + 1].to_broadcast([P, P]), ident_f32[:])
+                nc.scalar.copy(out=rate_by_col[:, :, in_bank * part : in_bank * (part + 1)],
+                               in_=bank[:].rearrange("p m q -> p q m"))
+            nc.scalar.activation(out=one_minus_rate[:], in_=rate[:], func=ACT.Copy, bias=1.0, scale=-1.0)
+
+        def new_operand(name):
+            codes = operand_pool.tile([P, B], U32, tag="codes", align_bytes=64, name=name + "_codes")
+            plane = operand_pool.tile([P, B], U8, tag="plane", align_bytes=64, name=name + "_plane")
             return codes, plane
 
-        def flip_x(step):
-            x_operands[step] = flip_and_quantise(x_chunks[step], ROUND_TILES, (nc.scalar.copy,))
-            if step + X_AHEAD < STEPS:
-                load_x(step + X_AHEAD)
-
-        def mx_pass(bank, operand, column, weight_words, weight_plane, start, stop):
+        def quantise(operand, grouped):
             codes, plane = operand
+            nc.vector.quantize_mx(out=codes[:].bitcast(FP8X4), scales=plane[:],
+                                  in_=grouped[:].rearrange("p i m t -> p (i m t)"))
+
+        def new_grouped():
+            return grouped_pool.tile([P, ROW_TILES, P, 4], BF16, tag="grouped", align_bytes=64, name="grouped")
+
+        def flip(operand, rows, g, copiers):
+            grouped = new_grouped()
+            for pair in range(2):
+                flipped = psum.tile([P, 2, 2, P], F32, tag="work")
+                for u in range(2):
+                    for j in range(2):
+                        words = rows[:, 2 * pair + j, :].bitcast(F32)
+                        nc.tensor.transpose(flipped[:, u, j, :],
+                                            words[:, WORDS_PASS * g + u : WORDS_PASS * (g + 1) : 2], ident_f32[:])
+                copiers[pair](
+                    out=grouped[:, 2 * pair : 2 * pair + 2, :, :].rearrange("p i m t -> p (i m t)").bitcast(F32),
+                    in_=flipped[:].rearrange("p u j m -> p (j m) u"),
+                )
+            quantise(operand, grouped)
+
+        def mx_pass(bank, stationary, moving, start, stop):
             nc.tensor.matmul_mx(
-                out=bank[:],
-                lhsT=codes[:, column : column + P].bitcast(FP8X4),
-                lhsT_scale=plane[:, column : column + P],
-                rhs=weight_words.bitcast(FP8X4),
-                rhs_scale=weight_plane,
-                start=start,
-                stop=stop,
+                out=bank,
+                lhsT=stationary[0].bitcast(FP8X4), lhsT_scale=stationary[1],
+                rhs=moving[0].bitcast(FP8X4), rhs_scale=moving[1],
+                start=start, stop=stop,
             )
 
-        def xin_passes(steps):
-            for j in range(ROUND_TILES):
-                for n_half in range(HALVES):
-                    if steps[0] % STEPS_ROUND == 0:
-                        xin[(j, n_half)] = psum.tile([P, HALF], F32, tag="sum", name="xin_%d_%d" % (j, n_half))
-                    for step in steps:
-                        part = step % STEPS_ROUND
-                        for k in range(STEP_GROUPS):
-                            g = STEP_GROUPS * part + k
-                            mx_pass(
-                                xin[(j, n_half)], x_operands[step], FLIP_COLS * k + P * j,
-                                win_words[:, g, half_cols(n_half)],
-                                win_planes[4 * k : P, part, half_cols(n_half)],
-                                start=(g == 0), stop=(g == GROUPS_IN - 1),
-                            )
+        def columns(operand, i):
+            codes, plane = operand
+            return codes[:, P * i : P * (i + 1)], plane[:, P * i : P * (i + 1)]
 
-        def normalise(i):
-            one = slice(i, i + 1)
-            nc.vector.scalar_tensor_tensor(out=z[:, i, :], in0=z[:, i, :], scalar=neg_mean[:, one], in1=gain[:],
-                                           op0=ALU.add, op1=ALU.mult)
-            nc.vector.scalar_tensor_tensor(out=z[:, i, :], in0=z[:, i, :], scalar=rstd[:, one], in1=shift[:],
-                                           op0=ALU.mult, op1=ALU.add)
-
-        def finish_round(rnd, result_pool):
-            def begin(j, n_half):
-                res = result_pool.tile([P, HALF], F32, tag="res")
-                nc.vector.tensor_tensor(out=res[:], in0=xin[(j, n_half)][:],
-                                        in1=z[:, ROUND_TILES * rnd + j, half_cols(n_half)], op=ALU.add)
-                nc.scalar.activation(out=res[:], in_=res[:], func=ACT.Tanh)
-                return res
-
-            def end(j, n_half, res):
-                i, cols = ROUND_TILES * rnd + j, half_cols(n_half)
-                nc.vector.tensor_tensor(out=res[:], in0=res[:], in1=rate[:, cols], op=ALU.mult)
-                nc.vector.tensor_tensor(out=res[:], in0=res[:], in1=h_rest[:, i, cols], op=ALU.add)
-                nc.sync.dma_start(out=out_rows[:, i, cols], in_=res[:])
-
-            banks = [(j, n_half) for j in range(ROUND_TILES) for n_half in range(HALVES)]
-            begun = begin(*banks[0])
-            for before, bank in zip(banks, banks[1:]):
-                following = begin(*bank)
-                end(*before, begun)
-                begun = following
-            end(*banks[-1], begun)
-
-        with tc.tile_pool(name="hidden", bufs=1) as hidden:
-            liq_sb = hidden.tile([P, ROW_TILES, H], BF16)
-            h_sb = hidden.tile([P, ROW_TILES, H], BF16)
-            v_sb = hidden.tile([P, ROW_TILES, H], BF16)
-            wv_words = hidden.tile([P, GROUPS_H, H], U32, align_bytes=64)
-            wo_words = hidden.tile([P, GROUPS_H, H], U32, align_bytes=64)
-            wv_planes = hidden.tile([P, H], U8, align_bytes=64)
-            wo_planes = hidden.tile([P, H], U8, align_bytes=64)
-            vec_rows = hidden.tile([P, H], BF16)
-            bv_all = hidden.tile([P, H], BF16)
-            bo_all = hidden.tile([P, H], BF16)
-            one_minus_rate = hidden.tile([P, H], F32)
-            squares = hidden.tile([P, H], BF16)
-
-            nc.vector.memset(vec_rows[:], 0.0)
-            nc.vector.memset(wv_planes[:].bitcast(I32), 0)
-            nc.vector.memset(wo_planes[:].bitcast(I32), 0)
-            nc.vector.memset(win_planes[:].rearrange("p s n -> p (s n)").bitcast(I32), 0)
-            nc.vector.memset(neg_half[:], -0.5)
-            make_identity(nc, ident_f32[:])
-            nc.vector.tensor_copy(out=ident_bf[:], in_=ident_f32[:])
-
-            def load_hidden_weight(words_sb, planes_sb, words, scales):
-                for quad in range(4):
-                    nc.sync.dma_start(out=planes_sb[32 * quad : 32 * quad + 4 * GROUPS_H, :].bitcast(I32),
-                                      in_=scales[:, 4 * quad : 4 * quad + 4, :].bitcast(I32))
-                nc.sync.dma_start(out=words_sb[:].bitcast(I32), in_=words_by_partition(words))
-
-            for row, vec in ((ROW_BV, b_v), (ROW_BO, b_o), (ROW_G, g_att), (ROW_BETA, beta_att),
-                             (ROW_BIN, b_in), (ROW_TAU, tau)):
-                nc.sync.dma_start(out=vec_rows[row : row + 1, :], in_=vec.rearrange("(o n) -> o n", o=1))
-            liq_rows = liq.rearrange("(p i) n -> p i n", i=ROW_TILES)
+        def permute_wv(wv_words, c):
+            cols = half_cols(c)
             for g in range(GROUPS_H):
-                nc.sync.dma_start(out=liq_sb[:, :, K_PASS * g : K_PASS * (g + 1)],
-                                  in_=liq_rows[:, :, K_PASS * g : K_PASS * (g + 1)])
-            load_hidden_weight(wv_words, wv_planes, W_v_words, W_v_scales)
-            load_x(0)
-            load_win(0)
-            load_hidden_weight(wo_words, wo_planes, W_o_words, W_o_scales)
-            load_x(1)
-            load_x(2)
-            load_win(1)
+                nc.vector.tensor_copy(
+                    out=wv_words_ctm[:, g, cols].bitcast(I32).rearrange("p (t m) -> p t m", t=4),
+                    in_=wv_words[:, g, cols].rearrange("p (m t) -> p t m", t=4),
+                )
+            nc.vector.tensor_copy(
+                out=wv_planes_ctm[:, cols].rearrange("p (t m) -> p t m", t=4),
+                in_=wv_planes[:, cols].rearrange("p (m t) -> p t m", t=4),
+            )
 
-            def spread(target, vector_rows, plus=0.0):
-                for n_half in range(HALVES):
-                    bank = psum.tile([P, HALF], F32, tag="sum")
-                    for count, row in enumerate(vector_rows):
-                        nc.tensor.matmul(
-                            out=bank[:],
-                            lhsT=ident_bf[:, row : row + 1].to_broadcast([P, P]),
-                            rhs=vec_rows[:, half_cols(n_half)],
-                            start=(count == 0),
-                            stop=(count == len(vector_rows) - 1),
-                        )
-                    nc.scalar.activation(out=target[:, half_cols(n_half)], in_=bank[:], func=ACT.Copy, bias=plus, scale=1.0)
-
-            def project_v(operand, n_half, tag):
-                cols = half_cols(n_half)
-                for i in range(ROW_TILES):
-                    bank = psum.tile([P, HALF], F32, tag=tag)
-                    for g in range(GROUPS_H):
-                        mx_pass(bank, operand, B * g + P * i, wv_words[:, g, cols],
-                                wv_planes[4 * g : P, cols], start=(g == 0), stop=(g == GROUPS_H - 1))
-                    nc.vector.tensor_tensor(out=v_sb[:, i, cols], in0=bank[:], in1=bv_all[:, cols], op=ALU.add)
-
-            def attend(i, operand):
-                for n_half in range(HALVES):
-                    cols = half_cols(n_half)
-                    bank = psum.tile([P, HALF], F32, tag="work")
-                    for g in range(GROUPS_H):
-                        mx_pass(bank, operand, B * g + P * i, wo_words[:, g, cols],
-                                wo_planes[4 * g : P, cols], start=(g == 0), stop=(g == GROUPS_H - 1))
-                    nc.vector.scalar_tensor_tensor(
-                        out=z[:, i, cols], in0=bank[:], scalar=1.0, in1=z[:, i, cols],
-                        op0=ALU.mult, op1=ALU.add, accum_out=row_sum[:, i, n_half : n_half + 1],
-                    )
-                nc.vector.tensor_scalar(out=neg_mean[:, i : i + 1], in0=row_sum[:, i, 0:1],
-                                        scalar1=row_sum[:, i, 1:2], scalar2=-1.0 / H, op0=ALU.add, op1=ALU.mult)
-
-            def deviation(i):
-                one = slice(i, i + 1)
-                nc.scalar.activation(out=squares[:], in_=z[:, i, :], func=ACT.Square, bias=neg_mean[:, one],
-                                     scale=1.0, accum_out=sq_sum[:, one])
-                nc.gpsimd.tensor_scalar(out=var_eps[:, one], in0=sq_sum[:, one], scalar1=1.0 / H, scalar2=LN_EPS,
-                                        op0=ALU.mult, op1=ALU.add)
-                nc.gpsimd.tensor_tensor(out=rstd[:, one], in0=var_eps[:, one], in1=neg_half[:], op=ALU.pow)
-
-            def rest_of_h(i):
-                nc.vector.tensor_tensor(out=h_rest[:, i, :], in0=h_sb[:, i, :], in1=one_minus_rate[:], op=ALU.mult)
-
-            spread(bv_all, [ROW_BV])
-            spread(bo_all, [ROW_BO])
-            liq_operand = flip_and_quantise(liq_sb, ROW_TILES, (nc.scalar.copy, nc.vector.tensor_copy))
-            spread(rate, [ROW_TAU], plus=TAU_EPS)
-            spread(gain, [ROW_G])
-            spread(shift, [ROW_BETA, ROW_BIN])
-            project_v(liq_operand, 0, "work")
-            project_v(liq_operand, 1, "sum")
-            flip_x(0)
-            load_win(2)
-            v_operand = flip_and_quantise(v_sb, ROW_TILES, (nc.scalar.copy, nc.vector.tensor_copy))
+        def project_v(operands, c, tag):
+            grouped = new_grouped()
             for i in range(ROW_TILES):
-                nc.vector.tensor_tensor(out=z[:, i, :], in0=liq_sb[:, i, :], in1=bo_all[:], op=ALU.add)
-            xin_passes((0,))
-            flip_x(1)
-            load_win(3)
-            nc.sync.dma_start(out=h_sb[:], in_=h.rearrange("(p i) n -> p i n", i=ROW_TILES))
-            attend(0, v_operand)
-            attend(1, v_operand)
-            flip_x(2)
-            deviation(0)
-            deviation(1)
-            nc.vector.reciprocal(out=rate[:], in_=rate[:])
-            nc.scalar.activation(out=one_minus_rate[:], in_=rate[:], func=ACT.Copy, bias=1.0, scale=-1.0)
-            xin_passes((1,))
-            attend(2, v_operand)
-            attend(3, v_operand)
-            normalise(0)
-            flip_x(3)
-            deviation(2)
-            deviation(3)
-            normalise(1)
-            xin_passes((2,))
-            rest_of_h(0)
-            rest_of_h(1)
+                bank = psum.tile([P, 4, P], F32, tag=tag)
+                for t in range(4):
+                    cols = slice(HALF * c + P * t, HALF * c + P * (t + 1))
+                    for g in range(GROUPS_H):
+                        mx_pass(bank[:, t, :], (wv_words_ctm[:, g, cols], wv_planes_ctm[4 * g : P, cols]),
+                                columns(operands[g], i), start=(g == 0), stop=(g == GROUPS_H - 1))
+                nc.vector.tensor_tensor(
+                    out=grouped[:, i, :, :], in0=bank[:].rearrange("p t m -> p m t"),
+                    in1=bv_sb[:, c, :].unsqueeze(1).to_broadcast([P, P, 4]), op=ALU.add,
+                )
+            return grouped
 
-            flip_x(4)
-            xin_passes((3,))
-            finish_round(0, results)
-            flip_x(5)
-            xin_passes((4,))
-            normalise(2)
-            rest_of_h(2)
-            flip_x(6)
-            xin_passes((5,))
-            normalise(3)
-            rest_of_h(3)
-            flip_x(7)
-            xin_passes((6, 7))
-            finish_round(1, results)
+        def attend(i):
+            for n_half in range(HALVES):
+                cols = half_cols(n_half)
+                bank = psum.tile([P, HALF], F32, tag="work")
+                for g in range(GROUPS_H):
+                    mx_pass(bank[:], columns(v_operands[g], i), (wo_words[:, g, cols], wo_planes[4 * g : P, cols]),
+                            start=(g == 0), stop=(g == GROUPS_H - 1))
+                nc.vector.scalar_tensor_tensor(
+                    out=z[:, i, cols], in0=bank[:], scalar=1.0, in1=z[:, i, cols],
+                    op0=ALU.mult, op1=ALU.add, accum_out=row_sum[:, i, n_half : n_half + 1],
+                )
+            nc.vector.tensor_scalar(out=neg_mean[:, i : i + 1], in0=row_sum[:, i, 0:1],
+                                    scalar1=row_sum[:, i, 1:2], scalar2=-1.0 / H, op0=ALU.add, op1=ALU.mult)
+
+        def deviation(i):
+            one = slice(i, i + 1)
+            nc.scalar.activation(out=vec_rows[:], in_=z[:, i, :], func=ACT.Square, bias=neg_mean[:, one],
+                                 scale=1.0, accum_out=sq_sum[:, one])
+            nc.gpsimd.tensor_scalar(out=var_eps[:, one], in0=sq_sum[:, one], scalar1=1.0 / H, scalar2=LN_EPS,
+                                    op0=ALU.mult, op1=ALU.add)
+            nc.gpsimd.tensor_tensor(out=rstd[:, one], in0=var_eps[:, one], in1=neg_half[:], op=ALU.pow)
+
+        def normalise(i, cols):
+            one = slice(i, i + 1)
+            nc.vector.scalar_tensor_tensor(out=z[:, i, cols], in0=z[:, i, cols], scalar=neg_mean[:, one],
+                                           in1=gain[:, cols], op0=ALU.add, op1=ALU.mult)
+            nc.vector.scalar_tensor_tensor(out=z[:, i, cols], in0=z[:, i, cols], scalar=rstd[:, one],
+                                           in1=shift[:, cols], op0=ALU.mult, op1=ALU.add)
+
+        def rest_of_h(i, cols):
+            nc.vector.tensor_tensor(out=h_rest[:, i, cols], in0=h_sb[:, i, cols], in1=one_minus_rate[:, cols],
+                                    op=ALU.mult)
+
+        def xin_pass(bank, i, g, cols):
+            planes = win_planes[4 * (g % PLANE_GROUPS) : P, g // PLANE_GROUPS, cols]
+            mx_pass(bank, columns(x_operands[g], i), (win_words[:, g, cols], planes),
+                    start=(g == 0), stop=(g == GROUPS_IN - 1))
+
+        def begin(bank, i, cols):
+            width = cols.stop - cols.start
+            res = results.tile([P, HALF], F32, tag="res")
+            nc.vector.tensor_tensor(out=res[:, 0:width], in0=bank, in1=z[:, i, cols], op=ALU.add)
+            nc.scalar.activation(out=res[:, 0:width], in_=res[:, 0:width], func=ACT.Tanh)
+            return res[:, 0:width], i, cols
+
+        def end(res, i, cols):
+            nc.vector.tensor_tensor(out=res, in0=res, in1=rate[:, cols], op=ALU.mult)
+            nc.vector.tensor_tensor(out=res, in0=res, in1=h_rest[:, i, cols], op=ALU.add)
+            nc.sync.dma_start(out=out_rows[:, i, cols], in_=res)
+
+        nc.vector.memset(vec_rows[:].bitcast(I32), 0)
+        nc.vector.memset(wv_planes[:].bitcast(I32), 0)
+        nc.vector.memset(win_planes[:].rearrange("p s n -> p (s n)").bitcast(I32), 0)
+        nc.vector.memset(wo_planes[:].bitcast(I32), 0)
+        nc.vector.memset(neg_half[:], -0.5)
+        make_identity(nc, ident_f32[:])
+        nc.vector.tensor_copy(out=ident_bf[:], in_=ident_f32[:])
+
+        liq_sb = new_rows("liq_sb")
+        for g in range(GROUPS_H):
+            nc.sync.dma_start(out=liq_sb[:, :, K_PASS * g : K_PASS * (g + 1)],
+                              in_=liq_rows[:, :, K_PASS * g : K_PASS * (g + 1)])
+            if g == 0:
+                for row, vec in ((ROW_BO, b_o), (ROW_G, g_att), (ROW_BETA, beta_att), (ROW_BIN, b_in)):
+                    nc.sync.dma_start(out=vec_rows[row : row + 1, :], in_=vec.rearrange("(o n) -> o n", o=1))
+                nc.sync.dma_start(out=tau_sb[:], in_=tau.rearrange("(p m) -> p m", m=TAU_COLS))
+        load_planes(wv_planes[:], W_v_scales)
+        wv_raw = new_rows("wv_raw")
+        wv_words = wv_raw[:].rearrange("p i n -> p (i n)").bitcast(I32).rearrange("p (g n) -> p g n", g=GROUPS_H)
+        nc.sync.dma_start(out=wv_words, in_=words_by_partition(W_v_words))
+        nc.gpsimd.dma_start(out=bv_sb[:], in_=b_v.rearrange("(c p t) -> p c t", p=P, t=4))
+        x_chunks = {0: load_x(0)}
+        load_win_planes(0)
+        load_win(0, 0)
+        load_planes(wo_planes[:], W_o_scales)
+        nc.sync.dma_start(out=wo_words[:].bitcast(I32), in_=words_by_partition(W_o_words))
+
+        idle_bank = psum.tile([P, P], F32, tag="sum")
+        for count in range(WARM_UP):
+            nc.tensor.matmul(out=idle_bank[:], lhsT=ident_bf[:], rhs=ident_bf[:], start=True, stop=True)
+        liq_operands = [new_operand("liq_%d" % g) for g in range(GROUPS_H)]
+        v_operands = [new_operand("v_%d" % g) for g in range(GROUPS_H)]
+        x_operands = [new_operand("x_%d" % g) for g in range(GROUPS_IN - 2 * GROUPS_H)]
+
+        def flip_x(g):
+            if g >= len(x_operands):
+                x_operands.append(new_operand("x_%d" % g))
+            flip(x_operands[g], x_chunks[g // CHUNK], g % CHUNK, (nc.scalar.copy, nc.scalar.copy))
+
+        def add_liq(i):
+            nc.vector.tensor_tensor(out=z[:, i, :], in0=liq_sb[:, i, :], in1=bo_all[:], op=ALU.add)
+
+        nc.vector.tensor_scalar(out=rate_cols[:], in0=tau_sb[:], scalar1=TAU_EPS, scalar2=None, op0=ALU.add)
+        nc.vector.reciprocal(out=rate_cols[:], in_=rate_cols[:])
+        spread(bo_all, [ROW_BO])
+        for g in range(GROUPS_H):
+            add_liq(g)
+            flip(liq_operands[g], liq_sb, g, (nc.scalar.copy, nc.scalar.copy))
+        permute_wv(wv_words, 0)
+        spread_rate()
+        spread(gain, [ROW_G])
+        spread(shift, [ROW_BETA, ROW_BIN])
+        permute_wv(wv_words, 1)
+        x_chunks[1] = load_x(1)
+        load_win(1, 0)
+        v_grouped = project_v(liq_operands, 0, "work")
+        quantise(v_operands[0], v_grouped)
+        add_liq(2)
+        flip_x(0)
+        add_liq(3)
+        flip_x(1)
+        v_grouped = project_v(liq_operands, 1, "sum")
+        quantise(v_operands[1], v_grouped)
+
+        first_half, second_half = half_cols(0), half_cols(1)
+        sums = [psum.tile([P, HALF], F32, tag="sum", name="sum_%d" % i) for i in range(ROW_TILES)]
+
+        def passes(g):
+            for i in range(ROW_TILES):
+                xin_pass(sums[i][:], i, g, first_half)
+
+        def more(chunk):
+            if chunk < CHUNKS:
+                x_chunks[chunk] = load_x(chunk)
+                if CHUNK * chunk % PLANE_GROUPS == 0:
+                    load_win_planes(CHUNK * chunk // PLANE_GROUPS)
+                load_win(chunk, 0)
+
+        chain = {
+            1: lambda: attend(0),
+            2: lambda: (deviation(0), attend(1)),
+            3: lambda: (deviation(1), attend(2)),
+            4: lambda: (deviation(2), attend(3), normalise(0, first_half)),
+            5: lambda: (deviation(3), normalise(1, first_half)),
+            6: lambda: normalise(2, first_half),
+            7: lambda: normalise(3, first_half),
+            8: lambda: (rest_of_h(0, first_half), rest_of_h(1, first_half)),
+            9: lambda: (rest_of_h(2, first_half), rest_of_h(3, first_half)),
+            10: lambda: normalise(0, second_half),
+            11: lambda: normalise(1, second_half),
+            12: lambda: normalise(2, second_half),
+            13: lambda: normalise(3, second_half),
+            14: lambda: (rest_of_h(0, second_half), rest_of_h(1, second_half)),
+            15: lambda: (rest_of_h(2, second_half), rest_of_h(3, second_half)),
+        }
+        more(2)
+        for g in range(GROUPS_IN):
+            if g + 2 < GROUPS_IN:
+                flip_x(g + 2)
+                if g % CHUNK == 1:
+                    more(g // CHUNK + 3)
+            if g == 4:
+                h_sb = new_rows("h_sb")
+                nc.sync.dma_start(out=h_sb[:], in_=h_rows)
+            passes(g)
+            if g in chain:
+                chain[g]()
+        for chunk in range(CHUNKS):
+            load_win(chunk, 1)
+        begun = None
+        for i in range(ROW_TILES):
+            following = begin(sums[i][:], i, first_half)
+            if begun is not None:
+                end(*begun)
+            begun = following
+        end(*begun)
+
+        last = ROW_TILES - 1
+        pieces = [(i, second_half, "work") for i in range(last)] + [
+            (last, slice(HALF, HALF + QUARTER), "work"), (last, slice(HALF + QUARTER, H), "sum")]
+        begun = None
+        for i, cols, tag in pieces:
+            width = cols.stop - cols.start
+            bank = psum.tile([P, HALF], F32, tag=tag)
+            for g in range(GROUPS_IN):
+                xin_pass(bank[:, 0:width], i, g, cols)
+            following = begin(bank[:, 0:width], i, cols)
+            if begun is not None:
+                end(*begun)
+            begun = following
+        end(*begun)

@@ -29,7 +29,7 @@ CHUNKS = GROUPS_IN // CHUNK
 PLANE_GROUPS = 4
 PLANE_SETS = GROUPS_IN // PLANE_GROUPS
 ROW_BUFFERS = 4
-WARM_UP = 8
+WARM_UP = 4
 TAU_COLS = H // P
 
 FLOPS = 2 * B * H * (IN + H + H)
@@ -59,6 +59,7 @@ def tile_advancedliquidneuralnetwork_pb_k_kernel(
         stack.enter_context(tc.manual_schedule())
         keep = stack.enter_context(tc.tile_pool(name="keep", bufs=1))
         rows_pool = stack.enter_context(tc.tile_pool(name="rows_pool", bufs=ROW_BUFFERS))
+        parted_pool = stack.enter_context(tc.tile_pool(name="parted_pool", bufs=2))
         grouped_pool = stack.enter_context(tc.tile_pool(name="grouped_pool", bufs=3))
         operand_pool = stack.enter_context(tc.tile_pool(name="operand_pool", bufs=GROUPS_IN))
         psum = stack.enter_context(tc.psum_pool(name="psum", bufs=4))
@@ -73,6 +74,7 @@ def tile_advancedliquidneuralnetwork_pb_k_kernel(
         wv_planes_ctm = keep.tile([P, H], U8, align_bytes=64)
         ident_f32 = keep.tile([P, P], F32)
         ident_bf = keep.tile([P, P], BF16)
+        pick_shift = keep.tile([P, 1], BF16)
         vec_rows = keep.tile([P, H], BF16)
         bv_sb = keep.tile([P, GROUPS_H, 4], BF16)
         tau_sb = keep.tile([P, TAU_COLS], BF16)
@@ -113,17 +115,11 @@ def tile_advancedliquidneuralnetwork_pb_k_kernel(
             nc.sync.dma_start(out=rows[:], in_=x_rows[:, :, H * chunk : H * (chunk + 1)])
             return rows
 
-        def spread(target, vector_rows):
+        def spread(target, picker):
             for n_half in range(HALVES):
                 bank = psum.tile([P, HALF], F32, tag="sum")
-                for count, row in enumerate(vector_rows):
-                    nc.tensor.matmul(
-                        out=bank[:],
-                        lhsT=ident_bf[:, row : row + 1].to_broadcast([P, P]),
-                        rhs=vec_rows[:, half_cols(n_half)],
-                        start=(count == 0),
-                        stop=(count == len(vector_rows) - 1),
-                    )
+                nc.tensor.matmul(out=bank[:], lhsT=picker.to_broadcast([P, P]), rhs=vec_rows[:, half_cols(n_half)],
+                                 start=True, stop=True)
                 nc.scalar.copy(out=target[:, half_cols(n_half)], in_=bank[:])
 
         def spread_rate():
@@ -151,15 +147,22 @@ def tile_advancedliquidneuralnetwork_pb_k_kernel(
         def new_grouped():
             return grouped_pool.tile([P, ROW_TILES, P, 4], BF16, tag="grouped", align_bytes=64, name="grouped")
 
-        def flip(operand, rows, g, copiers):
+        def every_second(rows, g):
+            return lambda i, u: rows[:, i, :].bitcast(F32)[:, WORDS_PASS * g + u : WORDS_PASS * (g + 1) : 2]
+
+        def part(rows, g, copier):
+            parted = parted_pool.tile([P, ROW_TILES, 2, P], F32, tag="parted", name="parted")
+            copier(out=parted[:],
+                   in_=rows[:, :, K_PASS * g : K_PASS * (g + 1)].bitcast(F32).rearrange("p i (m u) -> p i u m", u=2))
+            return lambda i, u: parted[:, i, u, :]
+
+        def flip(operand, words, copiers):
             grouped = new_grouped()
             for pair in range(2):
                 flipped = psum.tile([P, 2, 2, P], F32, tag="work")
                 for u in range(2):
                     for j in range(2):
-                        words = rows[:, 2 * pair + j, :].bitcast(F32)
-                        nc.tensor.transpose(flipped[:, u, j, :],
-                                            words[:, WORDS_PASS * g + u : WORDS_PASS * (g + 1) : 2], ident_f32[:])
+                        nc.tensor.transpose(flipped[:, u, j, :], words(2 * pair + j, u), ident_f32[:])
                 copiers[pair](
                     out=grouped[:, 2 * pair : 2 * pair + 2, :, :].rearrange("p i m t -> p (i m t)").bitcast(F32),
                     in_=flipped[:].rearrange("p u j m -> p (j m) u"),
@@ -255,6 +258,8 @@ def tile_advancedliquidneuralnetwork_pb_k_kernel(
             nc.vector.tensor_tensor(out=res, in0=res, in1=h_rest[:, i, cols], op=ALU.add)
             nc.sync.dma_start(out=out_rows[:, i, cols], in_=res)
 
+        zeros = z[:, 0, 0 : HALF // 2].bitcast(BF16)
+        nc.vector.memset(z[:, 0, 0 : HALF // 2], 0.0)
         nc.vector.memset(vec_rows[:].bitcast(I32), 0)
         nc.vector.memset(wv_planes[:].bitcast(I32), 0)
         nc.vector.memset(win_planes[:].rearrange("p s n -> p (s n)").bitcast(I32), 0)
@@ -262,62 +267,77 @@ def tile_advancedliquidneuralnetwork_pb_k_kernel(
         nc.vector.memset(neg_half[:], -0.5)
         make_identity(nc, ident_f32[:])
         nc.vector.tensor_copy(out=ident_bf[:], in_=ident_f32[:])
+        nc.vector.tensor_tensor(out=pick_shift[:], in0=ident_bf[:, ROW_BETA : ROW_BETA + 1],
+                                in1=ident_bf[:, ROW_BIN : ROW_BIN + 1], op=ALU.add)
 
+        wv_raw = new_rows("wv_raw")
+        wv_words = wv_raw[:].rearrange("p i n -> p (i n)").bitcast(I32).rearrange("p (g n) -> p g n", g=GROUPS_H)
         liq_sb = new_rows("liq_sb")
         for g in range(GROUPS_H):
             nc.sync.dma_start(out=liq_sb[:, :, K_PASS * g : K_PASS * (g + 1)],
                               in_=liq_rows[:, :, K_PASS * g : K_PASS * (g + 1)])
-            if g == 0:
-                for row, vec in ((ROW_BO, b_o), (ROW_G, g_att), (ROW_BETA, beta_att), (ROW_BIN, b_in)):
-                    nc.sync.dma_start(out=vec_rows[row : row + 1, :], in_=vec.rearrange("(o n) -> o n", o=1))
-                nc.sync.dma_start(out=tau_sb[:], in_=tau.rearrange("(p m) -> p m", m=TAU_COLS))
-        load_planes(wv_planes[:], W_v_scales)
-        wv_raw = new_rows("wv_raw")
-        wv_words = wv_raw[:].rearrange("p i n -> p (i n)").bitcast(I32).rearrange("p (g n) -> p g n", g=GROUPS_H)
+        for row, vec in ((ROW_BO, b_o), (ROW_G, g_att), (ROW_BETA, beta_att), (ROW_BIN, b_in)):
+            nc.sync.dma_start(out=vec_rows[row : row + 1, :], in_=vec.rearrange("(o n) -> o n", o=1))
+        nc.sync.dma_start(out=tau_sb[:], in_=tau.rearrange("(p m) -> p m", m=TAU_COLS))
         nc.sync.dma_start(out=wv_words, in_=words_by_partition(W_v_words))
+        load_planes(wv_planes[:], W_v_scales)
         nc.gpsimd.dma_start(out=bv_sb[:], in_=b_v.rearrange("(c p t) -> p c t", p=P, t=4))
         x_chunks = {0: load_x(0)}
         load_win_planes(0)
         load_win(0, 0)
+        x_chunks[1] = load_x(1)
         load_planes(wo_planes[:], W_o_scales)
         nc.sync.dma_start(out=wo_words[:].bitcast(I32), in_=words_by_partition(W_o_words))
+        load_win(1, 0)
 
-        idle_bank = psum.tile([P, P], F32, tag="sum")
+        idle_bank = psum.tile([P, HALF], F32, tag="sum")
         for count in range(WARM_UP):
-            nc.tensor.matmul(out=idle_bank[:], lhsT=ident_bf[:], rhs=ident_bf[:], start=True, stop=True)
+            nc.tensor.matmul(out=idle_bank[:], lhsT=zeros[:, 0:P], rhs=zeros, start=True, stop=True)
         liq_operands = [new_operand("liq_%d" % g) for g in range(GROUPS_H)]
         v_operands = [new_operand("v_%d" % g) for g in range(GROUPS_H)]
         x_operands = [new_operand("x_%d" % g) for g in range(GROUPS_IN - 2 * GROUPS_H)]
 
+        x_words = {}
+
+        def prepare(g):
+            rows, in_chunk = x_chunks[g // CHUNK], g % CHUNK
+            parted = g > 1 and g % 2 == 1
+            x_words[g] = part(rows, in_chunk, nc.scalar.copy) if parted else every_second(rows, in_chunk)
+
         def flip_x(g):
             if g >= len(x_operands):
                 x_operands.append(new_operand("x_%d" % g))
-            flip(x_operands[g], x_chunks[g // CHUNK], g % CHUNK, (nc.scalar.copy, nc.scalar.copy))
+            flip(x_operands[g], x_words[g], (nc.scalar.copy, nc.scalar.copy))
 
         def add_liq(i):
             nc.vector.tensor_tensor(out=z[:, i, :], in0=liq_sb[:, i, :], in1=bo_all[:], op=ALU.add)
 
+        def add_liq(i):
+            nc.vector.tensor_tensor(out=z[:, i, :], in0=liq_sb[:, i, :], in1=bo_all[:], op=ALU.add)
+
+        liq_words = [part(liq_sb, g, nc.vector.tensor_copy) for g in range(GROUPS_H)]
+        prepare(0)
+        prepare(1)
+        flip(liq_operands[0], liq_words[0], (nc.scalar.copy, nc.scalar.copy))
         nc.vector.tensor_scalar(out=rate_cols[:], in0=tau_sb[:], scalar1=TAU_EPS, scalar2=None, op0=ALU.add)
         nc.vector.reciprocal(out=rate_cols[:], in_=rate_cols[:])
-        spread(bo_all, [ROW_BO])
-        for g in range(GROUPS_H):
-            add_liq(g)
-            flip(liq_operands[g], liq_sb, g, (nc.scalar.copy, nc.scalar.copy))
         permute_wv(wv_words, 0)
-        spread_rate()
-        spread(gain, [ROW_G])
-        spread(shift, [ROW_BETA, ROW_BIN])
+        flip(liq_operands[1], liq_words[1], (nc.scalar.copy, nc.scalar.copy))
         permute_wv(wv_words, 1)
-        x_chunks[1] = load_x(1)
-        load_win(1, 0)
+        spread(bo_all, ident_bf[:, ROW_BO : ROW_BO + 1])
+        spread_rate()
+        spread(gain, ident_bf[:, ROW_G : ROW_G + 1])
         v_grouped = project_v(liq_operands, 0, "work")
         quantise(v_operands[0], v_grouped)
-        add_liq(2)
+        add_liq(0)
         flip_x(0)
-        add_liq(3)
+        spread(shift, pick_shift[:])
+        add_liq(1)
         flip_x(1)
         v_grouped = project_v(liq_operands, 1, "sum")
         quantise(v_operands[1], v_grouped)
+        add_liq(2)
+        add_liq(3)
 
         first_half, second_half = half_cols(0), half_cols(1)
         sums = [psum.tile([P, HALF], F32, tag="sum", name="sum_%d" % i) for i in range(ROW_TILES)]
@@ -350,8 +370,11 @@ def tile_advancedliquidneuralnetwork_pb_k_kernel(
             14: lambda: (rest_of_h(0, second_half), rest_of_h(1, second_half)),
             15: lambda: (rest_of_h(2, second_half), rest_of_h(3, second_half)),
         }
+        prepare(2)
         more(2)
         for g in range(GROUPS_IN):
+            if g + 3 < GROUPS_IN:
+                prepare(g + 3)
             if g + 2 < GROUPS_IN:
                 flip_x(g + 2)
                 if g % CHUNK == 1:

@@ -28,8 +28,8 @@ CHUNK = 2
 CHUNKS = GROUPS_IN // CHUNK
 PLANE_GROUPS = 4
 PLANE_SETS = GROUPS_IN // PLANE_GROUPS
-ROW_BUFFERS = 4
-WARM_UP = 4
+ROW_BUFFERS = 6
+WARM_UP = 6
 TAU_COLS = H // P
 
 FLOPS = 2 * B * H * (IN + H + H)
@@ -59,7 +59,6 @@ def tile_advancedliquidneuralnetwork_pb_k_kernel(
         stack.enter_context(tc.manual_schedule())
         keep = stack.enter_context(tc.tile_pool(name="keep", bufs=1))
         rows_pool = stack.enter_context(tc.tile_pool(name="rows_pool", bufs=ROW_BUFFERS))
-        parted_pool = stack.enter_context(tc.tile_pool(name="parted_pool", bufs=2))
         grouped_pool = stack.enter_context(tc.tile_pool(name="grouped_pool", bufs=3))
         operand_pool = stack.enter_context(tc.tile_pool(name="operand_pool", bufs=GROUPS_IN))
         psum = stack.enter_context(tc.psum_pool(name="psum", bufs=4))
@@ -67,10 +66,8 @@ def tile_advancedliquidneuralnetwork_pb_k_kernel(
 
         win_words = keep.tile([P, GROUPS_IN, H], U32, align_bytes=64)
         win_planes = keep.tile([P, PLANE_SETS, H], U8, align_bytes=64)
-        wo_words = keep.tile([P, GROUPS_H, H], U32, align_bytes=64)
         wv_planes = keep.tile([P, H], U8, align_bytes=64)
         wo_planes = keep.tile([P, H], U8, align_bytes=64)
-        wv_words_ctm = keep.tile([P, GROUPS_H, H], U32, align_bytes=64)
         wv_planes_ctm = keep.tile([P, H], U8, align_bytes=64)
         ident_f32 = keep.tile([P, P], F32)
         ident_bf = keep.tile([P, P], BF16)
@@ -110,6 +107,10 @@ def tile_advancedliquidneuralnetwork_pb_k_kernel(
         def new_rows(name):
             return rows_pool.tile([P, ROW_TILES, H], BF16, tag="rows", align_bytes=64, name=name)
 
+        def new_words(name):
+            rows = new_rows(name)
+            return rows[:].rearrange("p i n -> p (i n)").bitcast(U32).rearrange("p (g n) -> p g n", g=GROUPS_H)
+
         def load_x(chunk):
             rows = new_rows("x_%d" % chunk)
             nc.sync.dma_start(out=rows[:], in_=x_rows[:, :, H * chunk : H * (chunk + 1)])
@@ -147,22 +148,15 @@ def tile_advancedliquidneuralnetwork_pb_k_kernel(
         def new_grouped():
             return grouped_pool.tile([P, ROW_TILES, P, 4], BF16, tag="grouped", align_bytes=64, name="grouped")
 
-        def every_second(rows, g):
-            return lambda i, u: rows[:, i, :].bitcast(F32)[:, WORDS_PASS * g + u : WORDS_PASS * (g + 1) : 2]
-
-        def part(rows, g, copier):
-            parted = parted_pool.tile([P, ROW_TILES, 2, P], F32, tag="parted", name="parted")
-            copier(out=parted[:],
-                   in_=rows[:, :, K_PASS * g : K_PASS * (g + 1)].bitcast(F32).rearrange("p i (m u) -> p i u m", u=2))
-            return lambda i, u: parted[:, i, u, :]
-
-        def flip(operand, words, copiers):
+        def flip(operand, rows, g, copiers):
             grouped = new_grouped()
             for pair in range(2):
                 flipped = psum.tile([P, 2, 2, P], F32, tag="work")
                 for u in range(2):
                     for j in range(2):
-                        nc.tensor.transpose(flipped[:, u, j, :], words(2 * pair + j, u), ident_f32[:])
+                        words = rows[:, 2 * pair + j, :].bitcast(F32)
+                        nc.tensor.transpose(flipped[:, u, j, :],
+                                            words[:, WORDS_PASS * g + u : WORDS_PASS * (g + 1) : 2], ident_f32[:])
                 copiers[pair](
                     out=grouped[:, 2 * pair : 2 * pair + 2, :, :].rearrange("p i m t -> p (i m t)").bitcast(F32),
                     in_=flipped[:].rearrange("p u j m -> p (j m) u"),
@@ -181,12 +175,12 @@ def tile_advancedliquidneuralnetwork_pb_k_kernel(
             codes, plane = operand
             return codes[:, P * i : P * (i + 1)], plane[:, P * i : P * (i + 1)]
 
-        def permute_wv(wv_words, c):
+        def permute_wv(c):
             cols = half_cols(c)
             for g in range(GROUPS_H):
                 nc.vector.tensor_copy(
                     out=wv_words_ctm[:, g, cols].bitcast(I32).rearrange("p (t m) -> p t m", t=4),
-                    in_=wv_words[:, g, cols].rearrange("p (m t) -> p t m", t=4),
+                    in_=wv_words[:, g, cols].bitcast(I32).rearrange("p (m t) -> p t m", t=4),
                 )
             nc.vector.tensor_copy(
                 out=wv_planes_ctm[:, cols].rearrange("p (t m) -> p t m", t=4),
@@ -230,12 +224,13 @@ def tile_advancedliquidneuralnetwork_pb_k_kernel(
                                     op0=ALU.mult, op1=ALU.add)
             nc.gpsimd.tensor_tensor(out=rstd[:, one], in0=var_eps[:, one], in1=neg_half[:], op=ALU.pow)
 
-        def normalise(i, cols):
-            one = slice(i, i + 1)
-            nc.vector.scalar_tensor_tensor(out=z[:, i, cols], in0=z[:, i, cols], scalar=neg_mean[:, one],
-                                           in1=gain[:, cols], op0=ALU.add, op1=ALU.mult)
-            nc.vector.scalar_tensor_tensor(out=z[:, i, cols], in0=z[:, i, cols], scalar=rstd[:, one],
-                                           in1=shift[:, cols], op0=ALU.mult, op1=ALU.add)
+        def centre(i):
+            nc.vector.scalar_tensor_tensor(out=z[:, i, :], in0=z[:, i, :], scalar=neg_mean[:, i : i + 1],
+                                           in1=gain[:], op0=ALU.add, op1=ALU.mult)
+
+        def normalise(i):
+            nc.vector.scalar_tensor_tensor(out=z[:, i, :], in0=z[:, i, :], scalar=rstd[:, i : i + 1],
+                                           in1=shift[:], op0=ALU.mult, op1=ALU.add)
 
         def rest_of_h(i, cols):
             nc.vector.tensor_tensor(out=h_rest[:, i, cols], in0=h_sb[:, i, cols], in1=one_minus_rate[:, cols],
@@ -270,8 +265,8 @@ def tile_advancedliquidneuralnetwork_pb_k_kernel(
         nc.vector.tensor_tensor(out=pick_shift[:], in0=ident_bf[:, ROW_BETA : ROW_BETA + 1],
                                 in1=ident_bf[:, ROW_BIN : ROW_BIN + 1], op=ALU.add)
 
-        wv_raw = new_rows("wv_raw")
-        wv_words = wv_raw[:].rearrange("p i n -> p (i n)").bitcast(I32).rearrange("p (g n) -> p g n", g=GROUPS_H)
+        wv_words = new_words("wv_words")
+        wv_words_ctm = new_words("wv_words_ctm")
         liq_sb = new_rows("liq_sb")
         for g in range(GROUPS_H):
             nc.sync.dma_start(out=liq_sb[:, :, K_PASS * g : K_PASS * (g + 1)],
@@ -279,15 +274,16 @@ def tile_advancedliquidneuralnetwork_pb_k_kernel(
         for row, vec in ((ROW_BO, b_o), (ROW_G, g_att), (ROW_BETA, beta_att), (ROW_BIN, b_in)):
             nc.sync.dma_start(out=vec_rows[row : row + 1, :], in_=vec.rearrange("(o n) -> o n", o=1))
         nc.sync.dma_start(out=tau_sb[:], in_=tau.rearrange("(p m) -> p m", m=TAU_COLS))
-        nc.sync.dma_start(out=wv_words, in_=words_by_partition(W_v_words))
+        nc.sync.dma_start(out=wv_words.bitcast(I32), in_=words_by_partition(W_v_words))
         load_planes(wv_planes[:], W_v_scales)
         nc.gpsimd.dma_start(out=bv_sb[:], in_=b_v.rearrange("(c p t) -> p c t", p=P, t=4))
+        wo_words = new_words("wo_words")
         x_chunks = {0: load_x(0)}
         load_win_planes(0)
         load_win(0, 0)
         x_chunks[1] = load_x(1)
         load_planes(wo_planes[:], W_o_scales)
-        nc.sync.dma_start(out=wo_words[:].bitcast(I32), in_=words_by_partition(W_o_words))
+        nc.sync.dma_start(out=wo_words.bitcast(I32), in_=words_by_partition(W_o_words))
         load_win(1, 0)
 
         idle_bank = psum.tile([P, HALF], F32, tag="sum")
@@ -297,17 +293,10 @@ def tile_advancedliquidneuralnetwork_pb_k_kernel(
         v_operands = [new_operand("v_%d" % g) for g in range(GROUPS_H)]
         x_operands = [new_operand("x_%d" % g) for g in range(GROUPS_IN - 2 * GROUPS_H)]
 
-        x_words = {}
-
-        def prepare(g):
-            rows, in_chunk = x_chunks[g // CHUNK], g % CHUNK
-            parted = g > 1 and g % 2 == 1
-            x_words[g] = part(rows, in_chunk, nc.scalar.copy) if parted else every_second(rows, in_chunk)
-
         def flip_x(g):
             if g >= len(x_operands):
                 x_operands.append(new_operand("x_%d" % g))
-            flip(x_operands[g], x_words[g], (nc.scalar.copy, nc.scalar.copy))
+            flip(x_operands[g], x_chunks[g // CHUNK], g % CHUNK, (nc.scalar.copy, nc.scalar.copy))
 
         def add_liq(i):
             nc.vector.tensor_tensor(out=z[:, i, :], in0=liq_sb[:, i, :], in1=bo_all[:], op=ALU.add)
@@ -315,15 +304,12 @@ def tile_advancedliquidneuralnetwork_pb_k_kernel(
         def add_liq(i):
             nc.vector.tensor_tensor(out=z[:, i, :], in0=liq_sb[:, i, :], in1=bo_all[:], op=ALU.add)
 
-        liq_words = [part(liq_sb, g, nc.vector.tensor_copy) for g in range(GROUPS_H)]
-        prepare(0)
-        prepare(1)
-        flip(liq_operands[0], liq_words[0], (nc.scalar.copy, nc.scalar.copy))
+        flip(liq_operands[0], liq_sb, 0, (nc.scalar.copy, nc.scalar.copy))
         nc.vector.tensor_scalar(out=rate_cols[:], in0=tau_sb[:], scalar1=TAU_EPS, scalar2=None, op0=ALU.add)
         nc.vector.reciprocal(out=rate_cols[:], in_=rate_cols[:])
-        permute_wv(wv_words, 0)
-        flip(liq_operands[1], liq_words[1], (nc.scalar.copy, nc.scalar.copy))
-        permute_wv(wv_words, 1)
+        permute_wv(0)
+        flip(liq_operands[1], liq_sb, 1, (nc.scalar.copy, nc.scalar.copy))
+        permute_wv(1)
         spread(bo_all, ident_bf[:, ROW_BO : ROW_BO + 1])
         spread_rate()
         spread(gain, ident_bf[:, ROW_G : ROW_G + 1])
@@ -357,29 +343,24 @@ def tile_advancedliquidneuralnetwork_pb_k_kernel(
             1: lambda: attend(0),
             2: lambda: (deviation(0), attend(1)),
             3: lambda: (deviation(1), attend(2)),
-            4: lambda: (deviation(2), attend(3), normalise(0, first_half)),
-            5: lambda: (deviation(3), normalise(1, first_half)),
-            6: lambda: normalise(2, first_half),
-            7: lambda: normalise(3, first_half),
-            8: lambda: (rest_of_h(0, first_half), rest_of_h(1, first_half)),
-            9: lambda: (rest_of_h(2, first_half), rest_of_h(3, first_half)),
-            10: lambda: normalise(0, second_half),
-            11: lambda: normalise(1, second_half),
-            12: lambda: normalise(2, second_half),
-            13: lambda: normalise(3, second_half),
-            14: lambda: (rest_of_h(0, second_half), rest_of_h(1, second_half)),
-            15: lambda: (rest_of_h(2, second_half), rest_of_h(3, second_half)),
+            4: lambda: (deviation(2), attend(3)),
+            5: lambda: (deviation(3), centre(0)),
+            6: lambda: (centre(1), normalise(0)),
+            7: lambda: normalise(1),
+            8: lambda: centre(2),
+            9: lambda: centre(3),
+            10: lambda: normalise(2),
+            11: lambda: normalise(3),
+            12: lambda: (rest_of_h(0, first_half), rest_of_h(1, first_half)),
+            13: lambda: (rest_of_h(2, first_half), rest_of_h(3, first_half)),
         }
-        prepare(2)
         more(2)
         for g in range(GROUPS_IN):
-            if g + 3 < GROUPS_IN:
-                prepare(g + 3)
             if g + 2 < GROUPS_IN:
                 flip_x(g + 2)
                 if g % CHUNK == 1:
                     more(g // CHUNK + 3)
-            if g == 4:
+            if g == 6:
                 h_sb = new_rows("h_sb")
                 nc.sync.dma_start(out=h_sb[:], in_=h_rows)
             passes(g)
@@ -394,6 +375,9 @@ def tile_advancedliquidneuralnetwork_pb_k_kernel(
                 end(*begun)
             begun = following
         end(*begun)
+
+        for i in range(ROW_TILES):
+            rest_of_h(i, second_half)
 
         last = ROW_TILES - 1
         pieces = [(i, second_half, "work") for i in range(last)] + [

@@ -64,11 +64,11 @@ def tile_advancedliquidneuralnetwork_pb_k_kernel(
         psum = stack.enter_context(tc.psum_pool(name="psum", bufs=4))
         results = stack.enter_context(tc.tile_pool(name="results", bufs=4))
 
-        win_words = keep.tile([P, GROUPS_IN, H], U32, align_bytes=64)
-        win_planes = keep.tile([P, PLANE_SETS, H], U8, align_bytes=64)
-        wv_planes = keep.tile([P, H], U8, align_bytes=64)
-        wo_planes = keep.tile([P, H], U8, align_bytes=64)
-        wv_planes_ctm = keep.tile([P, H], U8, align_bytes=64)
+        win_words = keep.tile([P, GROUPS_IN, H], U32, align_bytes=256)
+        win_planes = keep.tile([P, PLANE_SETS, H], U8, align_bytes=256)
+        wv_planes = keep.tile([P, H], U8, align_bytes=256)
+        wo_planes = keep.tile([P, H], U8, align_bytes=256)
+        wv_planes_ctm = keep.tile([P, H], U8, align_bytes=256)
         ident_f32 = keep.tile([P, P], F32)
         ident_bf = keep.tile([P, P], BF16)
         pick_shift = keep.tile([P, 1], BF16)
@@ -105,7 +105,7 @@ def tile_advancedliquidneuralnetwork_pb_k_kernel(
                               in_=words_by_partition(W_in_words)[:, groups, half_cols(n_half)])
 
         def new_rows(name):
-            return rows_pool.tile([P, ROW_TILES, H], BF16, tag="rows", align_bytes=64, name=name)
+            return rows_pool.tile([P, ROW_TILES, H], BF16, tag="rows", align_bytes=256, name=name)
 
         def new_words(name):
             rows = new_rows(name)
@@ -136,8 +136,8 @@ def tile_advancedliquidneuralnetwork_pb_k_kernel(
             nc.scalar.activation(out=one_minus_rate[:], in_=rate[:], func=ACT.Copy, bias=1.0, scale=-1.0)
 
         def new_operand(name):
-            codes = operand_pool.tile([P, B], U32, tag="codes", align_bytes=64, name=name + "_codes")
-            plane = operand_pool.tile([P, B], U8, tag="plane", align_bytes=64, name=name + "_plane")
+            codes = operand_pool.tile([P, B], U32, tag="codes", align_bytes=256, name=name + "_codes")
+            plane = operand_pool.tile([P, B], U8, tag="plane", align_bytes=256, name=name + "_plane")
             return codes, plane
 
         def quantise(operand, grouped):
@@ -146,7 +146,7 @@ def tile_advancedliquidneuralnetwork_pb_k_kernel(
                                   in_=grouped[:].rearrange("p i m t -> p (i m t)"))
 
         def new_grouped():
-            return grouped_pool.tile([P, ROW_TILES, P, 4], BF16, tag="grouped", align_bytes=64, name="grouped")
+            return grouped_pool.tile([P, ROW_TILES, P, 4], BF16, tag="grouped", align_bytes=256, name="grouped")
 
         def flip(operand, rows, g, copiers):
             grouped = new_grouped()
@@ -297,9 +297,6 @@ def tile_advancedliquidneuralnetwork_pb_k_kernel(
             if g >= len(x_operands):
                 x_operands.append(new_operand("x_%d" % g))
             flip(x_operands[g], x_chunks[g // CHUNK], g % CHUNK, (nc.scalar.copy, nc.scalar.copy))
-
-        def add_liq(i):
-            nc.vector.tensor_tensor(out=z[:, i, :], in0=liq_sb[:, i, :], in1=bo_all[:], op=ALU.add)
 
         def add_liq(i):
             nc.vector.tensor_tensor(out=z[:, i, :], in0=liq_sb[:, i, :], in1=bo_all[:], op=ALU.add)

@@ -62,7 +62,7 @@ def tile_advancedliquidneuralnetwork_pb_k_kernel(
         grouped_pool = stack.enter_context(tc.tile_pool(name="grouped_pool", bufs=3))
         operand_pool = stack.enter_context(tc.tile_pool(name="operand_pool", bufs=GROUPS_IN))
         psum = stack.enter_context(tc.psum_pool(name="psum", bufs=4))
-        results = stack.enter_context(tc.tile_pool(name="results", bufs=4))
+        results = stack.enter_context(tc.tile_pool(name="results", bufs=6))
 
         win_words = keep.tile([P, GROUPS_IN, H], U32, align_bytes=256)
         win_planes = keep.tile([P, PLANE_SETS, H], U8, align_bytes=256)
@@ -148,7 +148,7 @@ def tile_advancedliquidneuralnetwork_pb_k_kernel(
         def new_grouped():
             return grouped_pool.tile([P, ROW_TILES, P, 4], BF16, tag="grouped", align_bytes=256, name="grouped")
 
-        def flip(operand, rows, g, copiers):
+        def flip(rows, g):
             grouped = new_grouped()
             for pair in range(2):
                 flipped = psum.tile([P, 2, 2, P], F32, tag="work")
@@ -157,11 +157,11 @@ def tile_advancedliquidneuralnetwork_pb_k_kernel(
                         words = rows[:, 2 * pair + j, :].bitcast(F32)
                         nc.tensor.transpose(flipped[:, u, j, :],
                                             words[:, WORDS_PASS * g + u : WORDS_PASS * (g + 1) : 2], ident_f32[:])
-                copiers[pair](
+                nc.scalar.copy(
                     out=grouped[:, 2 * pair : 2 * pair + 2, :, :].rearrange("p i m t -> p (i m t)").bitcast(F32),
                     in_=flipped[:].rearrange("p u j m -> p (j m) u"),
                 )
-            quantise(operand, grouped)
+            return grouped
 
         def mx_pass(bank, stationary, moving, start, stop):
             nc.tensor.matmul_mx(
@@ -179,12 +179,12 @@ def tile_advancedliquidneuralnetwork_pb_k_kernel(
             cols = half_cols(c)
             for g in range(GROUPS_H):
                 nc.vector.tensor_copy(
-                    out=wv_words_ctm[:, g, cols].bitcast(I32).rearrange("p (t m) -> p t m", t=4),
-                    in_=wv_words[:, g, cols].bitcast(I32).rearrange("p (m t) -> p t m", t=4),
+                    out=wv_words_ctm[:, g, cols].bitcast(I32).rearrange("p (t m) -> p m t", t=4),
+                    in_=wv_words[:, g, cols].bitcast(I32).rearrange("p (m t) -> p m t", t=4),
                 )
             nc.vector.tensor_copy(
-                out=wv_planes_ctm[:, cols].rearrange("p (t m) -> p t m", t=4),
-                in_=wv_planes[:, cols].rearrange("p (m t) -> p t m", t=4),
+                out=wv_planes_ctm[:, cols].rearrange("p (t m) -> p m t", t=4),
+                in_=wv_planes[:, cols].rearrange("p (m t) -> p m t", t=4),
             )
 
         def project_v(operands, c, tag):
@@ -232,9 +232,8 @@ def tile_advancedliquidneuralnetwork_pb_k_kernel(
             nc.vector.scalar_tensor_tensor(out=z[:, i, :], in0=z[:, i, :], scalar=rstd[:, i : i + 1],
                                            in1=shift[:], op0=ALU.mult, op1=ALU.add)
 
-        def rest_of_h(i, cols):
-            nc.vector.tensor_tensor(out=h_rest[:, i, cols], in0=h_sb[:, i, cols], in1=one_minus_rate[:, cols],
-                                    op=ALU.mult)
+        def rest_of_h(i):
+            nc.vector.tensor_tensor(out=h_rest[:, i, :], in0=h_sb[:, i, :], in1=one_minus_rate[:], op=ALU.mult)
 
         def xin_pass(bank, i, g, cols):
             planes = win_planes[4 * (g % PLANE_GROUPS) : P, g // PLANE_GROUPS, cols]
@@ -248,10 +247,22 @@ def tile_advancedliquidneuralnetwork_pb_k_kernel(
             nc.scalar.activation(out=res[:, 0:width], in_=res[:, 0:width], func=ACT.Tanh)
             return res[:, 0:width], i, cols
 
-        def end(res, i, cols):
+        def scale(res, i, cols):
             nc.vector.tensor_tensor(out=res, in0=res, in1=rate[:, cols], op=ALU.mult)
+
+        def end(res, i, cols):
             nc.vector.tensor_tensor(out=res, in0=res, in1=h_rest[:, i, cols], op=ALU.add)
             nc.sync.dma_start(out=out_rows[:, i, cols], in_=res)
+
+        def finish(banks):
+            pieces = []
+            for count in range(len(banks) + 2):
+                if count < len(banks):
+                    pieces.append(begin(*banks[count]))
+                if 1 <= count <= len(banks):
+                    scale(*pieces[count - 1])
+                if count >= 2:
+                    end(*pieces[count - 2])
 
         zeros = z[:, 0, 0 : HALF // 2].bitcast(BF16)
         nc.vector.memset(z[:, 0, 0 : HALF // 2], 0.0)
@@ -274,8 +285,11 @@ def tile_advancedliquidneuralnetwork_pb_k_kernel(
         for row, vec in ((ROW_BO, b_o), (ROW_G, g_att), (ROW_BETA, beta_att), (ROW_BIN, b_in)):
             nc.sync.dma_start(out=vec_rows[row : row + 1, :], in_=vec.rearrange("(o n) -> o n", o=1))
         nc.sync.dma_start(out=tau_sb[:], in_=tau.rearrange("(p m) -> p m", m=TAU_COLS))
-        nc.sync.dma_start(out=wv_words.bitcast(I32), in_=words_by_partition(W_v_words))
-        load_planes(wv_planes[:], W_v_scales)
+        for c in range(HALVES):
+            nc.sync.dma_start(out=wv_words[:, :, half_cols(c)].bitcast(I32),
+                              in_=words_by_partition(W_v_words)[:, :, half_cols(c)])
+            if c == 0:
+                load_planes(wv_planes[:], W_v_scales)
         nc.gpsimd.dma_start(out=bv_sb[:], in_=b_v.rearrange("(c p t) -> p c t", p=P, t=4))
         wo_words = new_words("wo_words")
         x_chunks = {0: load_x(0)}
@@ -296,16 +310,16 @@ def tile_advancedliquidneuralnetwork_pb_k_kernel(
         def flip_x(g):
             if g >= len(x_operands):
                 x_operands.append(new_operand("x_%d" % g))
-            flip(x_operands[g], x_chunks[g // CHUNK], g % CHUNK, (nc.scalar.copy, nc.scalar.copy))
+            return flip(x_chunks[g // CHUNK], g % CHUNK)
 
         def add_liq(i):
             nc.vector.tensor_tensor(out=z[:, i, :], in0=liq_sb[:, i, :], in1=bo_all[:], op=ALU.add)
 
-        flip(liq_operands[0], liq_sb, 0, (nc.scalar.copy, nc.scalar.copy))
         nc.vector.tensor_scalar(out=rate_cols[:], in0=tau_sb[:], scalar1=TAU_EPS, scalar2=None, op0=ALU.add)
         nc.vector.reciprocal(out=rate_cols[:], in_=rate_cols[:])
+        quantise(liq_operands[0], flip(liq_sb, 0))
         permute_wv(0)
-        flip(liq_operands[1], liq_sb, 1, (nc.scalar.copy, nc.scalar.copy))
+        quantise(liq_operands[1], flip(liq_sb, 1))
         permute_wv(1)
         spread(bo_all, ident_bf[:, ROW_BO : ROW_BO + 1])
         spread_rate()
@@ -313,12 +327,14 @@ def tile_advancedliquidneuralnetwork_pb_k_kernel(
         v_grouped = project_v(liq_operands, 0, "work")
         quantise(v_operands[0], v_grouped)
         add_liq(0)
-        flip_x(0)
+        x_grouped = [flip_x(0)]
+        quantise(x_operands[0], x_grouped[0])
         spread(shift, pick_shift[:])
-        add_liq(1)
-        flip_x(1)
+        x_grouped.append(flip_x(1))
         v_grouped = project_v(liq_operands, 1, "sum")
+        quantise(x_operands[1], x_grouped[1])
         quantise(v_operands[1], v_grouped)
+        add_liq(1)
         add_liq(2)
         add_liq(3)
 
@@ -339,22 +355,22 @@ def tile_advancedliquidneuralnetwork_pb_k_kernel(
         chain = {
             1: lambda: attend(0),
             2: lambda: (deviation(0), attend(1)),
-            3: lambda: (deviation(1), attend(2)),
-            4: lambda: (deviation(2), attend(3)),
-            5: lambda: (deviation(3), centre(0)),
-            6: lambda: (centre(1), normalise(0)),
-            7: lambda: normalise(1),
-            8: lambda: centre(2),
-            9: lambda: centre(3),
-            10: lambda: normalise(2),
-            11: lambda: normalise(3),
-            12: lambda: (rest_of_h(0, first_half), rest_of_h(1, first_half)),
-            13: lambda: (rest_of_h(2, first_half), rest_of_h(3, first_half)),
+            3: lambda: (deviation(1), attend(2), centre(0)),
+            4: lambda: (deviation(2), attend(3), normalise(0)),
+            5: lambda: (deviation(3), centre(1)),
+            6: lambda: (normalise(1), centre(2)),
+            7: lambda: (centre(3), normalise(2)),
+            8: lambda: normalise(3),
+            9: lambda: rest_of_h(0),
+            10: lambda: rest_of_h(1),
+            11: lambda: rest_of_h(2),
+            12: lambda: rest_of_h(3),
         }
         more(2)
         for g in range(GROUPS_IN):
             if g + 2 < GROUPS_IN:
-                flip_x(g + 2)
+                grouped = flip_x(g + 2)
+                quantise(x_operands[g + 2], grouped)
                 if g % CHUNK == 1:
                     more(g // CHUNK + 3)
             if g == 6:
@@ -365,28 +381,14 @@ def tile_advancedliquidneuralnetwork_pb_k_kernel(
                 chain[g]()
         for chunk in range(CHUNKS):
             load_win(chunk, 1)
-        begun = None
-        for i in range(ROW_TILES):
-            following = begin(sums[i][:], i, first_half)
-            if begun is not None:
-                end(*begun)
-            begun = following
-        end(*begun)
-
-        for i in range(ROW_TILES):
-            rest_of_h(i, second_half)
+        finish([(sums[i][:], i, first_half) for i in range(ROW_TILES)])
 
         last = ROW_TILES - 1
-        pieces = [(i, second_half, "work") for i in range(last)] + [
-            (last, slice(HALF, HALF + QUARTER), "work"), (last, slice(HALF + QUARTER, H), "sum")]
-        begun = None
-        for i, cols, tag in pieces:
-            width = cols.stop - cols.start
+        halves = [slice(HALF, HALF + QUARTER), slice(HALF + QUARTER, H)]
+        for i, cols, tag in [(i, second_half, "work") for i in range(last)] + [(last, halves[0], "work"), (last, halves[1], "sum")]:
             bank = psum.tile([P, HALF], F32, tag=tag)
             for g in range(GROUPS_IN):
-                xin_pass(bank[:, 0:width], i, g, cols)
-            following = begin(bank[:, 0:width], i, cols)
-            if begun is not None:
-                end(*begun)
-            begun = following
-        end(*begun)
+                xin_pass(bank[:, 0 : cols.stop - cols.start], i, g, cols)
+            step = P if cols == halves[1] else cols.stop - cols.start
+            finish([(bank[:, first - cols.start : first - cols.start + step], i, slice(first, first + step))
+                    for first in range(cols.start, cols.stop, step)])

@@ -389,6 +389,6 @@ def tile_advancedliquidneuralnetwork_pb_k_kernel(
             bank = psum.tile([P, HALF], F32, tag=tag)
             for g in range(GROUPS_IN):
                 xin_pass(bank[:, 0 : cols.stop - cols.start], i, g, cols)
-            step = P if cols == halves[1] else cols.stop - cols.start
+            step = (cols.stop - cols.start) // 2
             finish([(bank[:, first - cols.start : first - cols.start + step], i, slice(first, first + step))
                     for first in range(cols.start, cols.stop, step)])

@@ -29,6 +29,7 @@ CHUNKS = GROUPS_IN // CHUNK
 PLANE_GROUPS = 4
 PLANE_SETS = GROUPS_IN // PLANE_GROUPS
 ROW_BUFFERS = 6
+TOGETHER = 2
 WARM_UP = 6
 TAU_COLS = H // P
 
@@ -62,7 +63,6 @@ def tile_advancedliquidneuralnetwork_pb_k_kernel(
         grouped_pool = stack.enter_context(tc.tile_pool(name="grouped_pool", bufs=3))
         operand_pool = stack.enter_context(tc.tile_pool(name="operand_pool", bufs=GROUPS_IN))
         psum = stack.enter_context(tc.psum_pool(name="psum", bufs=4))
-        results = stack.enter_context(tc.tile_pool(name="results", bufs=6))
 
         win_words = keep.tile([P, GROUPS_IN, H], U32, align_bytes=256)
         win_planes = keep.tile([P, PLANE_SETS, H], U8, align_bytes=256)
@@ -241,11 +241,10 @@ def tile_advancedliquidneuralnetwork_pb_k_kernel(
                     start=(g == 0), stop=(g == GROUPS_IN - 1))
 
         def begin(bank, i, cols):
-            width = cols.stop - cols.start
-            res = results.tile([P, HALF], F32, tag="res")
-            nc.vector.tensor_tensor(out=res[:, 0:width], in0=bank, in1=z[:, i, cols], op=ALU.add)
-            nc.scalar.activation(out=res[:, 0:width], in_=res[:, 0:width], func=ACT.Tanh)
-            return res[:, 0:width], i, cols
+            res = z[:, i, cols]
+            nc.vector.tensor_tensor(out=res, in0=bank, in1=res, op=ALU.add)
+            nc.scalar.activation(out=res, in_=res, func=ACT.Tanh)
+            return res, i, cols
 
         def scale(res, i, cols):
             nc.vector.tensor_tensor(out=res, in0=res, in1=rate[:, cols], op=ALU.mult)
@@ -278,6 +277,7 @@ def tile_advancedliquidneuralnetwork_pb_k_kernel(
 
         wv_words = new_words("wv_words")
         wv_words_ctm = new_words("wv_words_ctm")
+        x_chunks = {0: new_rows("x_0")}
         liq_sb = new_rows("liq_sb")
         for g in range(GROUPS_H):
             nc.sync.dma_start(out=liq_sb[:, :, K_PASS * g : K_PASS * (g + 1)],
@@ -291,14 +291,13 @@ def tile_advancedliquidneuralnetwork_pb_k_kernel(
             if c == 0:
                 load_planes(wv_planes[:], W_v_scales)
         nc.gpsimd.dma_start(out=bv_sb[:], in_=b_v.rearrange("(c p t) -> p c t", p=P, t=4))
-        wo_words = new_words("wo_words")
-        x_chunks = {0: load_x(0)}
+        nc.sync.dma_start(out=x_chunks[0][:], in_=x_rows[:, :, 0:H])
         load_win_planes(0)
-        load_win(0, 0)
         x_chunks[1] = load_x(1)
+        load_win(0, 0)
+        wo_words = new_words("wo_words")
         load_planes(wo_planes[:], W_o_scales)
         nc.sync.dma_start(out=wo_words.bitcast(I32), in_=words_by_partition(W_o_words))
-        load_win(1, 0)
 
         idle_bank = psum.tile([P, HALF], F32, tag="sum")
         for count in range(WARM_UP):
@@ -348,9 +347,10 @@ def tile_advancedliquidneuralnetwork_pb_k_kernel(
         def more(chunk):
             if chunk < CHUNKS:
                 x_chunks[chunk] = load_x(chunk)
-                if CHUNK * chunk % PLANE_GROUPS == 0:
-                    load_win_planes(CHUNK * chunk // PLANE_GROUPS)
-                load_win(chunk, 0)
+            if chunk <= CHUNKS:
+                if CHUNK * (chunk - 1) % PLANE_GROUPS == 0 and chunk > 1:
+                    load_win_planes(CHUNK * (chunk - 1) // PLANE_GROUPS)
+                load_win(chunk - 1, 0)
 
         chain = {
             1: lambda: attend(0),
@@ -367,13 +367,14 @@ def tile_advancedliquidneuralnetwork_pb_k_kernel(
             12: lambda: rest_of_h(3),
         }
         more(2)
+        more(3)
         for g in range(GROUPS_IN):
             if g + 2 < GROUPS_IN:
                 grouped = flip_x(g + 2)
                 quantise(x_operands[g + 2], grouped)
-                if g % CHUNK == 1:
-                    more(g // CHUNK + 3)
-            if g == 6:
+                if g % CHUNK == 0:
+                    more(g // CHUNK + 4)
+            if g == 5:
                 h_sb = new_rows("h_sb")
                 nc.sync.dma_start(out=h_sb[:], in_=h_rows)
             passes(g)
@@ -385,10 +386,20 @@ def tile_advancedliquidneuralnetwork_pb_k_kernel(
 
         last = ROW_TILES - 1
         halves = [slice(HALF, HALF + QUARTER), slice(HALF + QUARTER, H)]
-        for i, cols, tag in [(i, second_half, "work") for i in range(last)] + [(last, halves[0], "work"), (last, halves[1], "sum")]:
-            bank = psum.tile([P, HALF], F32, tag=tag)
-            for g in range(GROUPS_IN):
-                xin_pass(bank[:, 0 : cols.stop - cols.start], i, g, cols)
+
+        def finish_in_two(bank, i, cols):
             step = (cols.stop - cols.start) // 2
             finish([(bank[:, first - cols.start : first - cols.start + step], i, slice(first, first + step))
                     for first in range(cols.start, cols.stop, step)])
+
+        together = [psum.tile([P, HALF], F32, tag="work", name="together_%d" % i) for i in range(TOGETHER)]
+        for g in range(GROUPS_IN):
+            for i in range(TOGETHER):
+                xin_pass(together[i][:], i, g, second_half)
+        for i in range(TOGETHER):
+            finish_in_two(together[i], i, second_half)
+        for i, cols, tag in [(i, second_half, "work") for i in range(TOGETHER, last)] + [(last, halves[0], "work"), (last, halves[1], "sum")]:
+            bank = psum.tile([P, HALF], F32, tag=tag)
+            for g in range(GROUPS_IN):
+                xin_pass(bank[:, 0 : cols.stop - cols.start], i, g, cols)
+            finish_in_two(bank, i, cols)

@@ -35,7 +35,7 @@ TAU_COLS = H // P
 
 FLOPS = 2 * B * H * (IN + H + H)
 
-ROW_BO, ROW_G, ROW_BETA, ROW_BIN = 0, 1, 2, 3
+ROW_G, ROW_BETA, ROW_BIN = 0, 1, 2
 
 
 def half_cols(n_half):
@@ -72,6 +72,7 @@ def tile_advancedliquidneuralnetwork_pb_k_kernel(
         ident_f32 = keep.tile([P, P], F32)
         ident_bf = keep.tile([P, P], BF16)
         pick_shift = keep.tile([P, 1], BF16)
+        bo_row = keep.tile([P, H], BF16)
         vec_rows = keep.tile([P, H], BF16)
         bv_sb = keep.tile([P, GROUPS_H, 4], BF16)
         tau_sb = keep.tile([P, TAU_COLS], BF16)
@@ -116,12 +117,12 @@ def tile_advancedliquidneuralnetwork_pb_k_kernel(
             nc.sync.dma_start(out=rows[:], in_=x_rows[:, :, H * chunk : H * (chunk + 1)])
             return rows
 
-        def spread(target, picker):
+        def spread(target, rows, picker, copy):
             for n_half in range(HALVES):
                 bank = psum.tile([P, HALF], F32, tag="sum")
-                nc.tensor.matmul(out=bank[:], lhsT=picker.to_broadcast([P, P]), rhs=vec_rows[:, half_cols(n_half)],
+                nc.tensor.matmul(out=bank[:], lhsT=picker.to_broadcast([P, P]), rhs=rows[:, half_cols(n_half)],
                                  start=True, stop=True)
-                nc.scalar.copy(out=target[:, half_cols(n_half)], in_=bank[:])
+                copy(out=target[:, half_cols(n_half)], in_=bank[:])
 
         def spread_rate():
             rate_by_col = rate[:].rearrange("p (q m) -> p q m", m=TAU_COLS)
@@ -133,7 +134,6 @@ def tile_advancedliquidneuralnetwork_pb_k_kernel(
                     nc.tensor.transpose(bank[:, m, :], rate_cols[:, col : col + 1].to_broadcast([P, P]), ident_f32[:])
                 nc.scalar.copy(out=rate_by_col[:, :, in_bank * part : in_bank * (part + 1)],
                                in_=bank[:].rearrange("p m q -> p q m"))
-            nc.scalar.activation(out=one_minus_rate[:], in_=rate[:], func=ACT.Copy, bias=1.0, scale=-1.0)
 
         def new_operand(name):
             codes = operand_pool.tile([P, B], U32, tag="codes", align_bytes=256, name=name + "_codes")
@@ -175,13 +175,16 @@ def tile_advancedliquidneuralnetwork_pb_k_kernel(
             codes, plane = operand
             return codes[:, P * i : P * (i + 1)], plane[:, P * i : P * (i + 1)]
 
-        def permute_wv(c):
+        def permute_words(c):
             cols = half_cols(c)
             for g in range(GROUPS_H):
                 nc.vector.tensor_copy(
                     out=wv_words_ctm[:, g, cols].bitcast(I32).rearrange("p (t m) -> p m t", t=4),
                     in_=wv_words[:, g, cols].bitcast(I32).rearrange("p (m t) -> p m t", t=4),
                 )
+
+        def permute_planes(c):
+            cols = half_cols(c)
             nc.vector.tensor_copy(
                 out=wv_planes_ctm[:, cols].rearrange("p (t m) -> p m t", t=4),
                 in_=wv_planes[:, cols].rearrange("p (m t) -> p m t", t=4),
@@ -265,8 +268,9 @@ def tile_advancedliquidneuralnetwork_pb_k_kernel(
 
         zeros = z[:, 0, 0 : HALF // 2].bitcast(BF16)
         nc.vector.memset(z[:, 0, 0 : HALF // 2], 0.0)
-        nc.vector.memset(vec_rows[:].bitcast(I32), 0)
+        nc.vector.memset(bo_row[:].bitcast(I32), 0)
         nc.vector.memset(wv_planes[:].bitcast(I32), 0)
+        nc.vector.memset(vec_rows[:].bitcast(I32), 0)
         nc.vector.memset(win_planes[:].rearrange("p s n -> p (s n)").bitcast(I32), 0)
         nc.vector.memset(wo_planes[:].bitcast(I32), 0)
         nc.vector.memset(neg_half[:], -0.5)
@@ -279,17 +283,28 @@ def tile_advancedliquidneuralnetwork_pb_k_kernel(
         wv_words_ctm = new_words("wv_words_ctm")
         x_chunks = {0: new_rows("x_0")}
         liq_sb = new_rows("liq_sb")
-        for g in range(GROUPS_H):
-            nc.sync.dma_start(out=liq_sb[:, :, K_PASS * g : K_PASS * (g + 1)],
-                              in_=liq_rows[:, :, K_PASS * g : K_PASS * (g + 1)])
-        for row, vec in ((ROW_BO, b_o), (ROW_G, g_att), (ROW_BETA, beta_att), (ROW_BIN, b_in)):
-            nc.sync.dma_start(out=vec_rows[row : row + 1, :], in_=vec.rearrange("(o n) -> o n", o=1))
-        nc.sync.dma_start(out=tau_sb[:], in_=tau.rearrange("(p m) -> p m", m=TAU_COLS))
-        for c in range(HALVES):
+
+        def load_row(rows, row, vec):
+            nc.sync.dma_start(out=rows[row : row + 1, :], in_=vec.rearrange("(o n) -> o n", o=1))
+
+        def load_wv(c):
             nc.sync.dma_start(out=wv_words[:, :, half_cols(c)].bitcast(I32),
                               in_=words_by_partition(W_v_words)[:, :, half_cols(c)])
-            if c == 0:
-                load_planes(wv_planes[:], W_v_scales)
+
+        def load_liq(g):
+            nc.sync.dma_start(out=liq_sb[:, :, K_PASS * g : K_PASS * (g + 1)],
+                              in_=liq_rows[:, :, K_PASS * g : K_PASS * (g + 1)])
+
+        load_liq(0)
+        load_row(bo_row, 0, b_o)
+        nc.sync.dma_start(out=tau_sb[:], in_=tau.rearrange("(p m) -> p m", m=TAU_COLS))
+        load_liq(1)
+        load_planes(wv_planes[:], W_v_scales)
+        load_wv(0)
+        load_row(vec_rows, ROW_G, g_att)
+        load_row(vec_rows, ROW_BETA, beta_att)
+        load_row(vec_rows, ROW_BIN, b_in)
+        load_wv(1)
         nc.gpsimd.dma_start(out=bv_sb[:], in_=b_v.rearrange("(c p t) -> p c t", p=P, t=4))
         nc.sync.dma_start(out=x_chunks[0][:], in_=x_rows[:, :, 0:H])
         load_win_planes(0)
@@ -314,21 +329,23 @@ def tile_advancedliquidneuralnetwork_pb_k_kernel(
         def add_liq(i):
             nc.vector.tensor_tensor(out=z[:, i, :], in0=liq_sb[:, i, :], in1=bo_all[:], op=ALU.add)
 
+        spread(bo_all, bo_row, ident_bf[:, 0:1], nc.vector.tensor_copy)
         nc.vector.tensor_scalar(out=rate_cols[:], in0=tau_sb[:], scalar1=TAU_EPS, scalar2=None, op0=ALU.add)
         nc.vector.reciprocal(out=rate_cols[:], in_=rate_cols[:])
+        for c in range(HALVES):
+            permute_planes(c)
         quantise(liq_operands[0], flip(liq_sb, 0))
-        permute_wv(0)
+        permute_words(0)
         quantise(liq_operands[1], flip(liq_sb, 1))
-        permute_wv(1)
-        spread(bo_all, ident_bf[:, ROW_BO : ROW_BO + 1])
+        permute_words(1)
         spread_rate()
-        spread(gain, ident_bf[:, ROW_G : ROW_G + 1])
+        spread(gain, vec_rows, ident_bf[:, ROW_G : ROW_G + 1], nc.scalar.copy)
         v_grouped = project_v(liq_operands, 0, "work")
         quantise(v_operands[0], v_grouped)
         add_liq(0)
         x_grouped = [flip_x(0)]
         quantise(x_operands[0], x_grouped[0])
-        spread(shift, pick_shift[:])
+        spread(shift, vec_rows, pick_shift[:], nc.scalar.copy)
         x_grouped.append(flip_x(1))
         v_grouped = project_v(liq_operands, 1, "sum")
         quantise(x_operands[1], x_grouped[1])
@@ -360,7 +377,7 @@ def tile_advancedliquidneuralnetwork_pb_k_kernel(
             5: lambda: (deviation(3), centre(1)),
             6: lambda: (normalise(1), centre(2)),
             7: lambda: (centre(3), normalise(2)),
-            8: lambda: normalise(3),
+            8: lambda: (normalise(3), nc.scalar.activation(out=one_minus_rate[:], in_=rate[:], func=ACT.Copy, bias=1.0, scale=-1.0)),
             9: lambda: rest_of_h(0),
             10: lambda: rest_of_h(1),
             11: lambda: rest_of_h(2),

@@ -35,7 +35,7 @@ TAU_COLS = H // P
 
 FLOPS = 2 * B * H * (IN + H + H)
 
-ROW_G, ROW_BETA, ROW_BIN = 0, 1, 2
+ROW_BETA, ROW_BIN = 0, 1
 
 
 def half_cols(n_half):
@@ -73,6 +73,7 @@ def tile_advancedliquidneuralnetwork_pb_k_kernel(
         ident_bf = keep.tile([P, P], BF16)
         pick_shift = keep.tile([P, 1], BF16)
         bo_row = keep.tile([P, H], BF16)
+        gain_row = keep.tile([P, H], BF16)
         vec_rows = keep.tile([P, H], BF16)
         bv_sb = keep.tile([P, GROUPS_H, 4], BF16)
         tau_sb = keep.tile([P, TAU_COLS], BF16)
@@ -270,6 +271,7 @@ def tile_advancedliquidneuralnetwork_pb_k_kernel(
         nc.vector.memset(z[:, 0, 0 : HALF // 2], 0.0)
         nc.vector.memset(bo_row[:].bitcast(I32), 0)
         nc.vector.memset(wv_planes[:].bitcast(I32), 0)
+        nc.vector.memset(gain_row[:].bitcast(I32), 0)
         nc.vector.memset(vec_rows[:].bitcast(I32), 0)
         nc.vector.memset(win_planes[:].rearrange("p s n -> p (s n)").bitcast(I32), 0)
         nc.vector.memset(wo_planes[:].bitcast(I32), 0)
@@ -295,18 +297,20 @@ def tile_advancedliquidneuralnetwork_pb_k_kernel(
             nc.sync.dma_start(out=liq_sb[:, :, K_PASS * g : K_PASS * (g + 1)],
                               in_=liq_rows[:, :, K_PASS * g : K_PASS * (g + 1)])
 
+        nc.sync.dma_start(out=tau_sb[:], in_=tau.rearrange("(p m) -> p m", m=TAU_COLS))
         load_liq(0)
         load_row(bo_row, 0, b_o)
-        nc.sync.dma_start(out=tau_sb[:], in_=tau.rearrange("(p m) -> p m", m=TAU_COLS))
         load_liq(1)
         load_planes(wv_planes[:], W_v_scales)
         load_wv(0)
-        load_row(vec_rows, ROW_G, g_att)
+        load_row(gain_row, 0, g_att)
         load_row(vec_rows, ROW_BETA, beta_att)
-        load_row(vec_rows, ROW_BIN, b_in)
         load_wv(1)
+        load_row(vec_rows, ROW_BIN, b_in)
         nc.gpsimd.dma_start(out=bv_sb[:], in_=b_v.rearrange("(c p t) -> p c t", p=P, t=4))
-        nc.sync.dma_start(out=x_chunks[0][:], in_=x_rows[:, :, 0:H])
+        for g in range(CHUNK):
+            cols = slice(K_PASS * g, K_PASS * (g + 1))
+            nc.sync.dma_start(out=x_chunks[0][:, :, cols], in_=x_rows[:, :, cols])
         load_win_planes(0)
         x_chunks[1] = load_x(1)
         load_win(0, 0)
@@ -332,14 +336,14 @@ def tile_advancedliquidneuralnetwork_pb_k_kernel(
         spread(bo_all, bo_row, ident_bf[:, 0:1], nc.vector.tensor_copy)
         nc.vector.tensor_scalar(out=rate_cols[:], in0=tau_sb[:], scalar1=TAU_EPS, scalar2=None, op0=ALU.add)
         nc.vector.reciprocal(out=rate_cols[:], in_=rate_cols[:])
-        for c in range(HALVES):
-            permute_planes(c)
+        permute_planes(0)
         quantise(liq_operands[0], flip(liq_sb, 0))
         permute_words(0)
         quantise(liq_operands[1], flip(liq_sb, 1))
+        permute_planes(1)
         permute_words(1)
         spread_rate()
-        spread(gain, vec_rows, ident_bf[:, ROW_G : ROW_G + 1], nc.scalar.copy)
+        spread(gain, gain_row, ident_bf[:, 0:1], nc.scalar.copy)
         v_grouped = project_v(liq_operands, 0, "work")
         quantise(v_operands[0], v_grouped)
         add_liq(0)

from contextlib import ExitStack

import concourse.mybir as mybir
from concourse.masks import make_identity

F32 = mybir.dt.float32
BF16 = mybir.dt.bfloat16
I32 = mybir.dt.int32
U32 = mybir.dt.uint32
U8 = mybir.dt.uint8
FP8X4 = mybir.dt.float8_e4m3fn_x4
ALU = mybir.AluOpType
ACT = mybir.ActivationFunctionType

P = 128
B, IN, H = 512, 8192, 1024
LN_EPS = 1e-5
TAU_EPS = 1e-6
ROW_TILES = B // P
K_PASS = 4 * P
WORDS_PASS = K_PASS // 2
HALF = 512
HALVES = H // HALF
QUARTER = HALF // 2
GROUPS_H = H // K_PASS
GROUPS_IN = IN // K_PASS
CHUNK = 2
CHUNKS = GROUPS_IN // CHUNK
PLANE_GROUPS = 4
PLANE_SETS = GROUPS_IN // PLANE_GROUPS
ROW_BUFFERS = 6
TOGETHER = 2
WARM_UP = 6
TAU_COLS = H // P

FLOPS = 2 * B * H * (IN + H + H)

ROW_BETA, ROW_BIN = 0, 1


def half_cols(n_half):
    return slice(HALF * n_half, HALF * (n_half + 1))


def words_by_partition(words):
    return words.rearrange("g p n t -> p g (n t)").bitcast(I32)


def tile_advancedliquidneuralnetwork_pb_k_kernel(
    tc, liq, h, x, W_in_words, W_in_scales, b_in, W_v_words, W_v_scales, b_v,
    W_o_words, W_o_scales, b_o, g_att, beta_att, tau, out,
):
    nc = tc.nc
    x_rows = x.rearrange("(p i) k -> p i k", i=ROW_TILES)
    liq_rows = liq.rearrange("(p i) n -> p i n", i=ROW_TILES)
    h_rows = h.rearrange("(p i) n -> p i n", i=ROW_TILES)
    out_rows = out.rearrange("(p i) n -> p i n", i=ROW_TILES)

    with ExitStack() as stack:
        stack.enter_context(tc.manual_schedule())
        keep = stack.enter_context(tc.tile_pool(name="keep", bufs=1))
        rows_pool = stack.enter_context(tc.tile_pool(name="rows_pool", bufs=ROW_BUFFERS))
        grouped_pool = stack.enter_context(tc.tile_pool(name="grouped_pool", bufs=3))
        operand_pool = stack.enter_context(tc.tile_pool(name="operand_pool", bufs=GROUPS_IN))
        psum = stack.enter_context(tc.psum_pool(name="psum", bufs=4))

        win_words = keep.tile([P, GROUPS_IN, H], U32, align_bytes=256)
        win_planes = keep.tile([P, PLANE_SETS, H], U8, align_bytes=256)
        wv_planes = keep.tile([P, H], U8, align_bytes=256)
        wo_planes = keep.tile([P, H], U8, align_bytes=256)
        wv_planes_ctm = keep.tile([P, H], U8, align_bytes=256)
        ident_f32 = keep.tile([P, P], F32)
        ident_bf = keep.tile([P, P], BF16)
        pick_shift = keep.tile([P, 1], BF16)
        bo_row = keep.tile([P, H], BF16)
        gain_row = keep.tile([P, H], BF16)
        vec_rows = keep.tile([P, H], BF16)
        bv_sb = keep.tile([P, GROUPS_H, 4], BF16)
        tau_sb = keep.tile([P, TAU_COLS], BF16)
        rate_cols = keep.tile([P, TAU_COLS], F32)
        bo_all = keep.tile([P, H], BF16)
        gain = keep.tile([P, H], BF16)
        shift = keep.tile([P, H], F32)
        rate = keep.tile([P, H], F32)
        one_minus_rate = keep.tile([P, H], F32)
        z = keep.tile([P, ROW_TILES, H], F32)
        h_rest = keep.tile([P, ROW_TILES, H], F32)
        row_sum = keep.tile([P, ROW_TILES, HALVES], F32)
        neg_mean = keep.tile([P, ROW_TILES], F32)
        sq_sum = keep.tile([P, ROW_TILES], F32)
        var_eps = keep.tile([P, ROW_TILES], F32)
        rstd = keep.tile([P, ROW_TILES], F32)
        neg_half = keep.tile([P, 1], F32)

        def load_planes(planes, scales):
            groups = scales.shape[0]
            for quad in range(4):
                nc.sync.dma_start(out=planes[32 * quad : 32 * quad + 4 * groups, :].bitcast(I32),
                                  in_=scales[:, 4 * quad : 4 * quad + 4, :].bitcast(I32))

        def load_win_planes(which):
            load_planes(win_planes[:, which, :], W_in_scales[PLANE_GROUPS * which : PLANE_GROUPS * (which + 1)])

        def load_win(chunk, n_half):
            groups = slice(CHUNK * chunk, CHUNK * (chunk + 1))
            nc.sync.dma_start(out=win_words[:, groups, half_cols(n_half)].bitcast(I32),
                              in_=words_by_partition(W_in_words)[:, groups, half_cols(n_half)])

        def new_rows(name):
            return rows_pool.tile([P, ROW_TILES, H], BF16, tag="rows", align_bytes=256, name=name)

        def new_words(name):
            rows = new_rows(name)
            return rows[:].rearrange("p i n -> p (i n)").bitcast(U32).rearrange("p (g n) -> p g n", g=GROUPS_H)

        def load_x(chunk):
            rows = new_rows("x_%d" % chunk)
            nc.sync.dma_start(out=rows[:], in_=x_rows[:, :, H * chunk : H * (chunk + 1)])
            return rows

        def spread(target, rows, picker, copy):
            for n_half in range(HALVES):
                bank = psum.tile([P, HALF], F32, tag="sum")
                nc.tensor.matmul(out=bank[:], lhsT=picker.to_broadcast([P, P]), rhs=rows[:, half_cols(n_half)],
                                 start=True, stop=True)
                copy(out=target[:, half_cols(n_half)], in_=bank[:])

        def spread_rate():
            rate_by_col = rate[:].rearrange("p (q m) -> p q m", m=TAU_COLS)
            in_bank = TAU_COLS // 2
            for part in range(2):
                bank = psum.tile([P, in_bank, P], F32, tag="sum")
                for m in range(in_bank):
                    col = in_bank * part + m
                    nc.tensor.transpose(bank[:, m, :], rate_cols[:, col : col + 1].to_broadcast([P, P]), ident_f32[:])
                nc.scalar.copy(out=rate_by_col[:, :, in_bank * part : in_bank * (part + 1)],
                               in_=bank[:].rearrange("p m q -> p q m"))

        def new_operand(name):
            codes = operand_pool.tile([P, B], U32, tag="codes", align_bytes=256, name=name + "_codes")
            plane = operand_pool.tile([P, B], U8, tag="plane", align_bytes=256, name=name + "_plane")
            return codes, plane

        def quantise(operand, grouped):
            codes, plane = operand
            nc.vector.quantize_mx(out=codes[:].bitcast(FP8X4), scales=plane[:],
                                  in_=grouped[:].rearrange("p i m t -> p (i m t)"))

        def new_grouped():
            return grouped_pool.tile([P, ROW_TILES, P, 4], BF16, tag="grouped", align_bytes=256, name="grouped")

        def flip(rows, g):
            grouped = new_grouped()
            for pair in range(2):
                flipped = psum.tile([P, 2, 2, P], F32, tag="work")
                for u in range(2):
                    for j in range(2):
                        words = rows[:, 2 * pair + j, :].bitcast(F32)
                        nc.tensor.transpose(flipped[:, u, j, :],
                                            words[:, WORDS_PASS * g + u : WORDS_PASS * (g + 1) : 2], ident_f32[:])
                nc.scalar.copy(
                    out=grouped[:, 2 * pair : 2 * pair + 2, :, :].rearrange("p i m t -> p (i m t)").bitcast(F32),
                    in_=flipped[:].rearrange("p u j m -> p (j m) u"),
                )
            return grouped

        def mx_pass(bank, stationary, moving, start, stop):
            nc.tensor.matmul_mx(
                out=bank,
                lhsT=stationary[0].bitcast(FP8X4), lhsT_scale=stationary[1],
                rhs=moving[0].bitcast(FP8X4), rhs_scale=moving[1],
                start=start, stop=stop,
            )

        def columns(operand, i):
            codes, plane = operand
            return codes[:, P * i : P * (i + 1)], plane[:, P * i : P * (i + 1)]

        def permute_words(c):
            cols = half_cols(c)
            for g in range(GROUPS_H):
                nc.vector.tensor_copy(
                    out=wv_words_ctm[:, g, cols].bitcast(I32).rearrange("p (t m) -> p m t", t=4),
                    in_=wv_words[:, g, cols].bitcast(I32).rearrange("p (m t) -> p m t", t=4),
                )

        def permute_planes(c):
            cols = half_cols(c)
            nc.vector.tensor_copy(
                out=wv_planes_ctm[:, cols].rearrange("p (t m) -> p m t", t=4),
                in_=wv_planes[:, cols].rearrange("p (m t) -> p m t", t=4),
            )

        def project_v(operands, c, tag):
            grouped = new_grouped()
            for i in range(ROW_TILES):
                bank = psum.tile([P, 4, P], F32, tag=tag)
                for t in range(4):
                    cols = slice(HALF * c + P * t, HALF * c + P * (t + 1))
                    for g in range(GROUPS_H):
                        mx_pass(bank[:, t, :], (wv_words_ctm[:, g, cols], wv_planes_ctm[4 * g : P, cols]),
                                columns(operands[g], i), start=(g == 0), stop=(g == GROUPS_H - 1))
                nc.vector.tensor_tensor(
                    out=grouped[:, i, :, :], in0=bank[:].rearrange("p t m -> p m t"),
                    in1=bv_sb[:, c, :].unsqueeze(1).to_broadcast([P, P, 4]), op=ALU.add,
                )
            return grouped

        def attend(i):
            for n_half in range(HALVES):
                cols = half_cols(n_half)
                bank = psum.tile([P, HALF], F32, tag="work")
                for g in range(GROUPS_H):
                    mx_pass(bank[:], columns(v_operands[g], i), (wo_words[:, g, cols], wo_planes[4 * g : P, cols]),
                            start=(g == 0), stop=(g == GROUPS_H - 1))
                nc.vector.scalar_tensor_tensor(
                    out=z[:, i, cols], in0=bank[:], scalar=1.0, in1=z[:, i, cols],
                    op0=ALU.mult, op1=ALU.add, accum_out=row_sum[:, i, n_half : n_half + 1],
                )
            nc.vector.tensor_scalar(out=neg_mean[:, i : i + 1], in0=row_sum[:, i, 0:1],
                                    scalar1=row_sum[:, i, 1:2], scalar2=-1.0 / H, op0=ALU.add, op1=ALU.mult)

        def deviation(i):
            one = slice(i, i + 1)
            nc.scalar.activation(out=vec_rows[:], in_=z[:, i, :], func=ACT.Square, bias=neg_mean[:, one],
                                 scale=1.0, accum_out=sq_sum[:, one])
            nc.gpsimd.tensor_scalar(out=var_eps[:, one], in0=sq_sum[:, one], scalar1=1.0 / H, scalar2=LN_EPS,
                                    op0=ALU.mult, op1=ALU.add)
            nc.gpsimd.tensor_tensor(out=rstd[:, one], in0=var_eps[:, one], in1=neg_half[:], op=ALU.pow)

        def centre(i):
            nc.vector.scalar_tensor_tensor(out=z[:, i, :], in0=z[:, i, :], scalar=neg_mean[:, i : i + 1],
                                           in1=gain[:], op0=ALU.add, op1=ALU.mult)

        def normalise(i):
            nc.vector.scalar_tensor_tensor(out=z[:, i, :], in0=z[:, i, :], scalar=rstd[:, i : i + 1],
                                           in1=shift[:], op0=ALU.mult, op1=ALU.add)

        def rest_of_h(i):
            nc.vector.tensor_tensor(out=h_rest[:, i, :], in0=h_sb[:, i, :], in1=one_minus_rate[:], op=ALU.mult)

        def xin_pass(bank, i, g, cols):
            planes = win_planes[4 * (g % PLANE_GROUPS) : P, g // PLANE_GROUPS, cols]
            mx_pass(bank, columns(x_operands[g], i), (win_words[:, g, cols], planes),
                    start=(g == 0), stop=(g == GROUPS_IN - 1))

        def begin(bank, i, cols):
            res = z[:, i, cols]
            nc.vector.tensor_tensor(out=res, in0=bank, in1=res, op=ALU.add)
            nc.scalar.activation(out=res, in_=res, func=ACT.Tanh)
            return res, i, cols

        def scale(res, i, cols):
            nc.vector.tensor_tensor(out=res, in0=res, in1=rate[:, cols], op=ALU.mult)

        def end(res, i, cols):
            nc.vector.tensor_tensor(out=res, in0=res, in1=h_rest[:, i, cols], op=ALU.add)
            nc.sync.dma_start(out=out_rows[:, i, cols], in_=res)

        def finish(banks):
            pieces = []
            for count in range(len(banks) + 2):
                if count < len(banks):
                    pieces.append(begin(*banks[count]))
                if 1 <= count <= len(banks):
                    scale(*pieces[count - 1])
                if count >= 2:
                    end(*pieces[count - 2])

        zeros = z[:, 0, 0 : HALF // 2].bitcast(BF16)
        nc.vector.memset(z[:, 0, 0 : HALF // 2], 0.0)
        nc.vector.memset(bo_row[:].bitcast(I32), 0)
        nc.vector.memset(wv_planes[:].bitcast(I32), 0)
        nc.vector.memset(gain_row[:].bitcast(I32), 0)
        nc.vector.memset(vec_rows[:].bitcast(I32), 0)
        nc.vector.memset(win_planes[:].rearrange("p s n -> p (s n)").bitcast(I32), 0)
        nc.vector.memset(wo_planes[:].bitcast(I32), 0)
        nc.vector.memset(neg_half[:], -0.5)
        make_identity(nc, ident_f32[:])
        nc.vector.tensor_copy(out=ident_bf[:], in_=ident_f32[:])
        nc.vector.tensor_tensor(out=pick_shift[:], in0=ident_bf[:, ROW_BETA : ROW_BETA + 1],
                                in1=ident_bf[:, ROW_BIN : ROW_BIN + 1], op=ALU.add)

        wv_words = new_words("wv_words")
        wv_words_ctm = new_words("wv_words_ctm")
        x_chunks = {0: new_rows("x_0")}
        liq_sb = new_rows("liq_sb")

        def load_row(rows, row, vec):
            nc.sync.dma_start(out=rows[row : row + 1, :], in_=vec.rearrange("(o n) -> o n", o=1))

        def load_wv(c):
            nc.sync.dma_start(out=wv_words[:, :, half_cols(c)].bitcast(I32),
                              in_=words_by_partition(W_v_words)[:, :, half_cols(c)])

        def load_liq(g):
            nc.sync.dma_start(out=liq_sb[:, :, K_PASS * g : K_PASS * (g + 1)],
                              in_=liq_rows[:, :, K_PASS * g : K_PASS * (g + 1)])

        nc.sync.dma_start(out=tau_sb[:], in_=tau.rearrange("(p m) -> p m", m=TAU_COLS))
        load_liq(0)
        load_row(bo_row, 0, b_o)
        load_liq(1)
        load_planes(wv_planes[:], W_v_scales)
        load_wv(0)
        load_row(gain_row, 0, g_att)
        load_row(vec_rows, ROW_BETA, beta_att)
        load_wv(1)
        load_row(vec_rows, ROW_BIN, b_in)
        nc.gpsimd.dma_start(out=bv_sb[:], in_=b_v.rearrange("(c p t) -> p c t", p=P, t=4))
        for g in range(CHUNK):
            cols = slice(K_PASS * g, K_PASS * (g + 1))
            nc.sync.dma_start(out=x_chunks[0][:, :, cols], in_=x_rows[:, :, cols])
        load_win_planes(0)
        x_chunks[1] = load_x(1)
        load_win(0, 0)
        wo_words = new_words("wo_words")
        load_planes(wo_planes[:], W_o_scales)
        nc.sync.dma_start(out=wo_words.bitcast(I32), in_=words_by_partition(W_o_words))

        idle_bank = psum.tile([P, HALF], F32, tag="sum")
        for count in range(WARM_UP):
            nc.tensor.matmul(out=idle_bank[:], lhsT=zeros[:, 0:P], rhs=zeros, start=True, stop=True)
        liq_operands = [new_operand("liq_%d" % g) for g in range(GROUPS_H)]
        v_operands = [new_operand("v_%d" % g) for g in range(GROUPS_H)]
        x_operands = [new_operand("x_%d" % g) for g in range(GROUPS_IN - 2 * GROUPS_H)]

        def flip_x(g):
            if g >= len(x_operands):
                x_operands.append(new_operand("x_%d" % g))
            return flip(x_chunks[g // CHUNK], g % CHUNK)

        def add_liq(i):
            nc.vector.tensor_tensor(out=z[:, i, :], in0=liq_sb[:, i, :], in1=bo_all[:], op=ALU.add)

        spread(bo_all, bo_row, ident_bf[:, 0:1], nc.vector.tensor_copy)
        nc.vector.tensor_scalar(out=rate_cols[:], in0=tau_sb[:], scalar1=TAU_EPS, scalar2=None, op0=ALU.add)
        nc.vector.reciprocal(out=rate_cols[:], in_=rate_cols[:])
        permute_planes(0)
        quantise(liq_operands[0], flip(liq_sb, 0))
        permute_words(0)
        quantise(liq_operands[1], flip(liq_sb, 1))
        permute_planes(1)
        permute_words(1)
        spread_rate()
        spread(gain, gain_row, ident_bf[:, 0:1], nc.scalar.copy)
        v_grouped = project_v(liq_operands, 0, "work")
        quantise(v_operands[0], v_grouped)
        add_liq(0)
        x_grouped = [flip_x(0)]
        quantise(x_operands[0], x_grouped[0])
        spread(shift, vec_rows, pick_shift[:], nc.scalar.copy)
        x_grouped.append(flip_x(1))
        v_grouped = project_v(liq_operands, 1, "sum")
        quantise(x_operands[1], x_grouped[1])
        quantise(v_operands[1], v_grouped)
        add_liq(1)
        add_liq(2)
        add_liq(3)

        first_half, second_half = half_cols(0), half_cols(1)
        sums = [psum.tile([P, HALF], F32, tag="sum", name="sum_%d" % i) for i in range(ROW_TILES)]

        def passes(g):
            for i in range(ROW_TILES):
                xin_pass(sums[i][:], i, g, first_half)

        def more(chunk):
            if chunk < CHUNKS:
                x_chunks[chunk] = load_x(chunk)
            if chunk <= CHUNKS:
                if CHUNK * (chunk - 1) % PLANE_GROUPS == 0 and chunk > 1:
                    load_win_planes(CHUNK * (chunk - 1) // PLANE_GROUPS)
                load_win(chunk - 1, 0)

        chain = {
            1: lambda: attend(0),
            2: lambda: (deviation(0), attend(1)),
            3: lambda: (deviation(1), attend(2), centre(0)),
            4: lambda: (deviation(2), attend(3), normalise(0)),
            5: lambda: (deviation(3), centre(1)),
            6: lambda: (normalise(1), centre(2)),
            7: lambda: (centre(3), normalise(2)),
            8: lambda: (normalise(3), nc.scalar.activation(out=one_minus_rate[:], in_=rate[:], func=ACT.Copy, bias=1.0, scale=-1.0)),
            9: lambda: rest_of_h(0),
            10: lambda: rest_of_h(1),
            11: lambda: rest_of_h(2),
            12: lambda: rest_of_h(3),
        }
        more(2)
        more(3)
        for g in range(GROUPS_IN):
            if g + 2 < GROUPS_IN:
                grouped = flip_x(g + 2)
                quantise(x_operands[g + 2], grouped)
                if g % CHUNK == 0:
                    more(g // CHUNK + 4)
            if g == 5:
                h_sb = new_rows("h_sb")
                nc.sync.dma_start(out=h_sb[:], in_=h_rows)
            passes(g)
            if g in chain:
                chain[g]()
        for chunk in range(CHUNKS):
            load_win(chunk, 1)
        finish([(sums[i][:], i, first_half) for i in range(ROW_TILES)])

        last = ROW_TILES - 1
        halves = [slice(HALF, HALF + QUARTER), slice(HALF + QUARTER, H)]

        def finish_in_two(bank, i, cols):
            step = (cols.stop - cols.start) // 2
            finish([(bank[:, first - cols.start : first - cols.start + step], i, slice(first, first + step))
                    for first in range(cols.start, cols.stop, step)])

        together = [psum.tile([P, HALF], F32, tag="work", name="together_%d" % i) for i in range(TOGETHER)]
        for g in range(GROUPS_IN):
            for i in range(TOGETHER):
                xin_pass(together[i][:], i, g, second_half)
        for i in range(TOGETHER):
            finish_in_two(together[i], i, second_half)
        for i, cols, tag in [(i, second_half, "work") for i in range(TOGETHER, last)] + [(last, halves[0], "work"), (last, halves[1], "sum")]:
            bank = psum.tile([P, HALF], F32, tag=tag)
            for g in range(GROUPS_IN):
                xin_pass(bank[:, 0 : cols.stop - cols.start], i, g, cols)
            finish_in_two(bank, i, cols)
